import numpy as np
import ml_dtypes


def mxq(x, axis, fmt="e4m3"):
    dtype, down = {"e4m3": (ml_dtypes.float8_e4m3fn, 7), "e5m2": (ml_dtypes.float8_e5m2, 14)}[fmt]
    v = np.moveaxis(np.asarray(x, np.float32).astype(ml_dtypes.bfloat16).astype(np.float64), axis, -1)
    blocks = v.reshape(v.shape[:-1] + (-1, 32))
    amax = np.abs(blocks).max(-1, keepdims=True)
    byte = np.maximum(np.where(amax > 0, np.frexp(amax)[1] - 1 + 127, 0) - down, 1)
    scale = np.exp2(byte - 127.0)
    codes = (blocks / scale).astype(np.float32).astype(dtype).astype(np.float64)
    return np.moveaxis((codes * scale).reshape(v.shape), -1, axis)


WIDE = False


def mx_kscale(k):
    if not WIDE:
        return np.ones(k)
    levels = np.array([10, -10, 5, -5, 0])
    a = np.random.permutation(np.resize(levels, k // 512 * 4)).reshape(k // 512, 4)
    idx = np.arange(k)
    return np.exp2(a[idx // 512, idx % 128 // 32])


BF16 = ml_dtypes.bfloat16


def bf(x):
    return np.asarray(x, np.float32).astype(BF16)


def f64(x):
    return np.asarray(x).astype(np.float64)


E2M1 = np.array([0.0, 0.5, 1.0, 1.5, 2.0, 3.0, 4.0, 6.0, -0.0, -0.5, -1.0, -1.5, -2.0, -3.0, -4.0, -6.0])


def pack_weight(w, fmt):
    k, n = w.shape
    w = f64(bf(w)).reshape(k // 32, 32, n)
    amax = np.abs(w).max(1)
    if fmt == "e4m3":
        byte = np.frexp(amax)[1] - 1 + 127 - 7
    else:
        mant, ex = np.frexp(amax / 6.0)
        byte = np.where(mant > 0.5, ex, ex - 1) + 127
    byte = np.clip(np.where(amax > 0, byte, 1), 1, 254)
    scaled = (w * np.exp2(127.0 - byte)[:, None, :]).reshape(k, n).astype(np.float32)
    by_word = np.ascontiguousarray(scaled.reshape(k // 512, 128, 4, n).transpose(0, 1, 3, 2))
    if fmt == "e4m3":
        words = by_word.astype(ml_dtypes.float8_e4m3fn).view(np.uint8)
    else:
        c = by_word.astype(ml_dtypes.float4_e2m1fn).view(np.uint8) & 0xF
        words = c[..., 0::2] | (c[..., 1::2] << 4)
    return np.ascontiguousarray(words), np.ascontiguousarray(byte.astype(np.uint8).reshape(k // 512, 16, n))


def unpack_weight(words, scales, fmt):
    g, p, n, _ = words.shape
    if fmt == "e4m3":
        vals = np.ascontiguousarray(words).view(ml_dtypes.float8_e4m3fn).astype(np.float64)
    else:
        nib = np.empty((g, p, n, 4), np.uint8)
        nib[..., 0::2] = words & 0xF
        nib[..., 1::2] = words >> 4
        vals = E2M1[nib]
    vals = vals * np.repeat(np.exp2(scales.astype(np.float64) - 127.0), 8, axis=1)[..., None]
    return vals.transpose(0, 1, 3, 2).reshape(g * 512, n)


B, N, C, L = 16, 16, 1024, 2
EPS = 1e-5
FMT = "e4m3"


def sigmoid(v):
    return 1.0 / (1.0 + np.exp(-v))


def bn(t, w, o):
    mean = t.mean(axis=(0, -1), keepdims=True)
    var = np.square(t - mean).mean(axis=(0, -1), keepdims=True)
    return (t - mean) / np.sqrt(var + EPS) * w[None, :, None] + o[None, :, None]


def setup_inputs():
    s = mx_kscale(C)

    def wx(g):
        w = np.random.standard_normal((C, C)) * g / np.sqrt(C) / s[None, :]
        return pack_weight(np.ascontiguousarray(w.T), FMT)

    x = bf(np.random.standard_normal((B, N, C)) * s)
    edge = bf(np.random.standard_normal((B, N * N, C)) * 1.5)
    Wu_words, Wu_scales = wx(0.5)
    Wv_words, Wv_scales = wx(6.0)
    Wa_words, Wa_scales = wx(1.0)
    Wb_words, Wb_scales = wx(1.0)
    We_words, We_scales = pack_weight(np.ascontiguousarray((np.random.standard_normal((C, C)) / np.sqrt(C)).T), FMT)
    return {
        "x": x,
        "edge": edge,
        "Wu_words": Wu_words,
        "Wu_scales": Wu_scales,
        "Wv_words": Wv_words,
        "Wv_scales": Wv_scales,
        "Wa_words": Wa_words,
        "Wa_scales": Wa_scales,
        "Wb_words": Wb_words,
        "Wb_scales": Wb_scales,
        "We_words": We_words,
        "We_scales": We_scales,
        "bnv_w": bf(1.0 + 0.1 * np.random.standard_normal(N)),
        "bnv_b": bf(0.1 * np.random.standard_normal(N)),
        "bne_w": bf(1.0 + 0.1 * np.random.standard_normal(N * N)),
        "bne_b": bf(0.1 * np.random.standard_normal(N * N)),
    }


def reference(x, edge, Wu_words, Wu_scales, Wv_words, Wv_scales, Wa_words, Wa_scales, Wb_words, Wb_scales, We_words, We_scales, bnv_w, bnv_b, bne_w, bne_b):
    edge = f64(edge)
    xq = mxq(f64(x).reshape(B * N, C), 1, "e4m3")
    ax = (xq @ unpack_weight(Wa_words, Wa_scales, FMT)).reshape(B, N, C)
    bx = (xq @ unpack_weight(Wb_words, Wb_scales, FMT)).reshape(B, N, C)
    ee = (mxq(edge.reshape(B * N * N, C), 1, "e4m3") @ unpack_weight(We_words, We_scales, FMT)).reshape(B, N * N, C)
    m = np.repeat(ax, N, axis=1) + np.tile(bx, (1, N, 1)) + ee
    edge_new = edge + np.maximum(bn(m, f64(bne_w), f64(bne_b)), 0.0)
    g = sigmoid(edge_new).reshape(B * N, N, C)
    p = np.exp(g - g.max(axis=1, keepdims=True))
    p = (p / p.sum(axis=1, keepdims=True)).reshape(B, N * N, C)
    vx = (xq @ unpack_weight(Wv_words, Wv_scales, FMT)).reshape(B, N, C)
    agg = (p * np.tile(vx, (1, N, 1))).reshape(B * N, N, C).sum(axis=1).reshape(B, N, C)
    y = (xq @ unpack_weight(Wu_words, Wu_scales, FMT)).reshape(B, N, C) + agg / N
    x_new = y + np.maximum(bn(y, f64(bnv_w), f64(bnv_b)), 0.0)
    return (x_new, edge_new)

@@ -1,0 +1,391 @@
+from contextlib import ExitStack
+
+import concourse.mybir as mybir
+from concourse.masks import make_identity
+
+F32 = mybir.dt.float32
+BF16 = mybir.dt.bfloat16
+I32 = mybir.dt.int32
+U8 = mybir.dt.uint8
+FP8X4 = mybir.dt.float8_e4m3fn_x4
+ALU = mybir.AluOpType
+ACT = mybir.ActivationFunctionType
+AX = mybir.AxisListType
+
+P = 128
+N = 16
+C = 1024
+HALVES = 2
+BL = 8
+G = 2
+BANK = 512
+QUARTERS = 4
+EPS = 1e-5
+COUNT = 16 * C
+
+MM_BANKS = 3
+VV_BANKS = 2
+PREFETCH = 4
+REP = 8
+
+FLOPS = 2 * C * C * (16 * 256 + 4 * 16 * 16)
+
+
+def tile_gnn_s2_pa_t_kernel(
+    tc,
+    x,
+    edge,
+    Wu_words,
+    Wu_scales,
+    Wv_words,
+    Wv_scales,
+    Wa_words,
+    Wa_scales,
+    Wb_words,
+    Wb_scales,
+    We_words,
+    We_scales,
+    bnv_w,
+    bnv_b,
+    bne_w,
+    bne_b,
+    out_0,
+    out_1,
+):
+    nc = tc.nc
+    edge_v = edge.rearrange("(h l) (i j) c -> h i l (j c)", l=BL, j=N)
+    out1_v = out_1.rearrange("(h l) (i j) c -> h i l (j c)", l=BL, j=N)
+    out0_v = out_0.rearrange("(h l) i c -> h i l c", l=BL)
+
+    with ExitStack() as ctx:
+        ctx.enter_context(tc.manual_schedule())
+        keep = ctx.enter_context(tc.tile_pool(name="keep", bufs=1))
+        edge_pool = ctx.enter_context(tc.tile_pool(name="edge", bufs=PREFETCH + 2))
+        group_pool = ctx.enter_context(tc.tile_pool(name="group", bufs=2))
+        code_pool = ctx.enter_context(tc.tile_pool(name="code", bufs=3))
+        work_pool = ctx.enter_context(tc.tile_pool(name="work", bufs=3))
+        junk_pool = ctx.enter_context(tc.tile_pool(name="junk", bufs=2))
+        small_pool = ctx.enter_context(tc.tile_pool(name="small", bufs=3))
+        tp_pool = ctx.enter_context(tc.psum_pool(name="tp", bufs=2))
+        mm_pool = ctx.enter_context(tc.psum_pool(name="mm", bufs=MM_BANKS))
+        vv_pool = ctx.enter_context(tc.psum_pool(name="vv", bufs=VV_BANKS))
+        sp_pool = ctx.enter_context(tc.psum_pool(name="sp", bufs=1))
+
+        def load_weight(words, scales, label):
+            codes = keep.tile([P, G, C], I32, name=label + "_codes", align_bytes=64)
+            plane = keep.tile([P, G, C], U8, name=label + "_plane", align_bytes=64)
+            nc.vector.memset(plane[:].rearrange("p g n -> p (g n)").bitcast(I32), 0)
+            for quad in range(4):
+                nc.sync.dma_start(
+                    out=plane[32 * quad : 32 * quad + 4, :, :].bitcast(I32),
+                    in_=scales[:, 4 * quad : 4 * quad + 4, :].rearrange("g r n -> r g n").bitcast(I32),
+                )
+            nc.sync.dma_start(out=codes[:], in_=words.rearrange("g p n t -> p g (n t)").bitcast(I32))
+            return codes, plane
+
+        edge_tiles = {}
+
+        def load_edge(j):
+            if j not in range(N):
+                return
+            et = edge_pool.tile([P, HALVES, C], BF16, name="et")
+            for half in range(HALVES):
+                nc.sync.dma_start(out=et[:, half, :], in_=edge_v[half, :, :, j * C : (j + 1) * C])
+            edge_tiles[j] = et
+
+        x_sb = keep.tile([P, HALVES, C], BF16, name="x_sb")
+        nc.sync.dma_start(out=x_sb[:], in_=x.rearrange("(h l) n c -> (l n) h c", l=BL))
+        wa = load_weight(Wa_words, Wa_scales, "wa")
+        load_edge(0)
+        we = load_weight(We_words, We_scales, "we")
+        wb = load_weight(Wb_words, Wb_scales, "wb")
+        for j in range(1, PREFETCH):
+            load_edge(j)
+        wv = load_weight(Wv_words, Wv_scales, "wv")
+        wu = load_weight(Wu_words, Wu_scales, "wu")
+
+        gain = keep.tile([P, N + 1], F32, name="gain")
+        shift = keep.tile([P, N + 1], F32, name="shift")
+        for dst, by_edge, by_node, label in ((gain, bne_w, bnv_w, "w"), (shift, bne_b, bnv_b, "b")):
+            e_bf = keep.tile([P, N], BF16, name="bne_" + label)
+            v_bf = keep.tile([P, 1], BF16, name="bnv_" + label)
+            nc.scalar.dma_start(
+                out=e_bf[:], in_=by_edge.rearrange("(i j) -> i j", j=N).unsqueeze(1).to_broadcast([N, BL, N])
+            )
+            nc.scalar.dma_start(
+                out=v_bf[:], in_=by_node.rearrange("(i o) -> i o", o=1).unsqueeze(1).to_broadcast([N, BL, 1])
+            )
+            nc.vector.tensor_copy(out=dst[:, 0:N], in_=e_bf[:])
+            nc.vector.tensor_copy(out=dst[:, N : N + 1], in_=v_bf[:])
+
+        warm = keep.tile([P, 1], F32, name="warm")
+        nc.vector.memset(warm[:], 0.0)
+        nc.scalar.activation(out=warm[:], in_=warm[:], func=ACT.Tanh)
+
+        ident = keep.tile([P, P], F32, name="ident")
+        make_identity(nc, ident[:])
+        same_i = keep.tile([P, N], F32, name="same_i")
+        nc.vector.tensor_reduce(
+            out=same_i[:], in_=ident[:].rearrange("p (i l) -> p i l", l=BL), axis=AX.X, op=ALU.add
+        )
+        group_mean = keep.tile([P, N, BL], F32, name="group_mean")
+        nc.vector.tensor_scalar_mul(
+            out=group_mean[:], in0=same_i[:].unsqueeze(2).to_broadcast([P, N, BL]), scalar1=-1.0 / COUNT
+        )
+        minus_half = keep.tile([P, 1], F32, name="minus_half")
+        nc.vector.memset(minus_half[:], -0.5)
+        stats = keep.tile([P, N + 1, 16], F32, name="stats")
+        nc.vector.memset(stats[:], 0.0)
+
+        def transpose_words(bank, rows):
+            words = rows.bitcast(F32)
+            for g in range(G):
+                for u in range(2):
+                    nc.tensor.transpose(
+                        out=bank[:, g, u, :], in_=words[:, 256 * g + u : 256 * (g + 1) : 2], identity=ident[:]
+                    )
+
+        xg = keep.tile([P, G * HALVES * P * 4], BF16, name="xg", align_bytes=64)
+        xg_words = xg[:].bitcast(F32).rearrange("p (g h n l u) -> p g h n l u", g=G, h=HALVES, n=N, l=BL)
+        for half in range(HALVES):
+            bank = tp_pool.tile([P, G, 2, P], F32, name="bank")
+            transpose_words(bank, x_sb[:, half, :])
+            for g in range(G):
+                nc.vector.tensor_copy(
+                    out=xg_words[:, g, half], in_=bank[:, g].rearrange("p u (l n) -> p n l u", l=BL)
+                )
+        xq = keep.tile([P, G * HALVES * P], I32, name="xq", align_bytes=64)
+        xs = keep.tile([P, G * HALVES * P], U8, name="xs", align_bytes=64)
+        nc.vector.memset(xs[:].bitcast(I32), 0)
+        nc.vector.quantize_mx(out=xq[:].bitcast(FP8X4), scales=xs[:], in_=xg[:])
+
+        xr = keep.tile([P, N, G * HALVES * P], I32, name="xr", align_bytes=64)
+        xrs = keep.tile([P, N, G * HALVES * P], U8, name="xrs", align_bytes=64)
+        xq_v = xq[:].rearrange("p (a n l) -> p n a l", a=G * HALVES, n=N)
+        xs_v = xs[:].bitcast(I32).rearrange("p (a n w) -> p n a w", a=G * HALVES, n=N)
+
+        def repeat_nodes(block):
+            if block not in range(N // REP):
+                return
+            js = slice(block * REP, (block + 1) * REP)
+            nc.vector.tensor_copy(
+                out=xr[:, js, :].rearrange("p j (a i l) -> p j a i l", a=G * HALVES, i=N),
+                in_=xq_v[:, js].unsqueeze(3).to_broadcast([P, REP, G * HALVES, N, BL]),
+            )
+            nc.vector.tensor_copy(
+                out=xrs[:, js, :].bitcast(I32).rearrange("p j (a i w) -> p j a i w", a=G * HALVES, i=N),
+                in_=xs_v[:, js].unsqueeze(3).to_broadcast([P, REP, G * HALVES, N, 2]),
+            )
+
+        def mx_passes(acc, stationary, weights, cols, first, last):
+            s_codes, s_plane = stationary
+            w_codes, w_plane = weights
+            for g in range(G):
+                nc.tensor.matmul_mx(
+                    out=acc[:],
+                    lhsT=s_codes(g).bitcast(FP8X4),
+                    lhsT_scale=s_plane(g),
+                    rhs=w_codes[:, g, cols].bitcast(FP8X4),
+                    rhs_scale=w_plane[:, g, cols],
+                    start=first and g == 0,
+                    stop=last and g == G - 1,
+                )
+
+        def block_of(codes, plane, half):
+            def cut(t):
+                return lambda g: t[:, (g * HALVES + half) * P : (g * HALVES + half + 1) * P]
+
+            return cut(codes), cut(plane)
+
+        def columns(k):
+            return slice((k % 2) * BANK, (k % 2 + 1) * BANK)
+
+        ax = keep.tile([P, HALVES, C], F32, name="ax")
+        for k in range(QUARTERS):
+            acc = mm_pool.tile([P, BANK], F32, name="acc")
+            mx_passes(acc, block_of(xq, xs, k // 2), wa, columns(k), True, True)
+            nc.scalar.copy(out=ax[:, k // 2, columns(k)], in_=acc[:])
+
+        groups = {}
+        codes = {}
+        banks = {}
+        values = {}
+        msgs = {}
+        gates = {}
+        coeffs = {}
+        den = keep.tile([P, HALVES, C], F32, name="den")
+        num = keep.tile([P, HALVES, C], F32, name="num")
+
+        def transpose_edge(j):
+            if j not in range(N):
+                return
+            eg = group_pool.tile([P, G * HALVES * P * 4], BF16, name="eg", align_bytes=64)
+            eg_words = eg[:].bitcast(F32).rearrange("p (g h r u) -> p g h r u", g=G, h=HALVES, u=2)
+            for half in range(HALVES):
+                bank = tp_pool.tile([P, G, 2, P], F32, name="bank")
+                transpose_words(bank, edge_tiles[j][:, half, :])
+                nc.scalar.copy(out=eg_words[:, :, half], in_=bank[:].rearrange("p g u r -> p g r u"))
+            groups[j] = eg
+
+        def quantise_edge(j):
+            if j not in range(N):
+                return
+            eq = code_pool.tile([P, G * HALVES * P], I32, name="eq", align_bytes=64)
+            es = code_pool.tile([P, G * HALVES * P], U8, name="es", align_bytes=64)
+            nc.vector.quantize_mx(out=eq[:].bitcast(FP8X4), scales=es[:], in_=groups[j][:])
+            codes[j] = (eq, es)
+
+        def fill_message_bank(q):
+            if q not in range(N * QUARTERS):
+                return
+            j, k = divmod(q, QUARTERS)
+            acc = mm_pool.tile([P, BANK], F32, name="acc")
+            mx_passes(acc, block_of(codes[j][0], codes[j][1], k // 2), we, columns(k), True, False)
+            mx_passes(acc, block_of(xr[:, j, :], xrs[:, j, :], k // 2), wb, columns(k), False, True)
+            banks[q] = acc
+
+        def evacuate(j, k):
+            if j not in range(N):
+                return
+            if k == 0:
+                msgs[j] = work_pool.tile([P, HALVES, C], F32, name="msg")
+            nc.vector.scalar_tensor_tensor(
+                out=msgs[j][:, k // 2, columns(k)],
+                in0=banks[QUARTERS * j + k][:],
+                scalar=1.0,
+                in1=ax[:, k // 2, columns(k)],
+                op0=ALU.mult,
+                op1=ALU.add,
+                accum_out=stats[:, j, k : k + 1],
+            )
+
+        def square_sum(values_tile, row):
+            junk = junk_pool.tile([P, HALVES, C], BF16, name="junk")
+            nc.scalar.activation(out=junk[:], in_=values_tile[:], func=ACT.Square, accum_out=stats[:, row, 8:9])
+
+        def stat_sums(row):
+            sums = sp_pool.tile([P, 16], F32, name="sums")
+            nc.tensor.matmul(
+                out=sums[:], lhsT=group_mean[:].rearrange("p i l -> p (i l)"), rhs=stats[:, row, :], start=True, stop=True
+            )
+            return sums
+
+        def coefficients(sums, row):
+            neg = small_pool.tile([P, 2], F32, name="neg")
+            nc.vector.tensor_reduce(out=neg[:], in_=sums[:].rearrange("p (a b) -> p a b", a=2), axis=AX.X, op=ALU.add)
+            nvar = small_pool.tile([P, 1], F32, name="nvar")
+            nc.gpsimd.tensor_scalar(
+                out=nvar[:], in0=neg[:, 0:1], scalar1=neg[:, 0:1], scalar2=neg[:, 1:2], op0=ALU.mult, op1=ALU.add
+            )
+            vpe = small_pool.tile([P, 1], F32, name="vpe")
+            nc.gpsimd.tensor_scalar(out=vpe[:], in0=nvar[:], scalar1=-1.0, scalar2=EPS, op0=ALU.mult, op1=ALU.add)
+            safe = small_pool.tile([P, 1], F32, name="safe")
+            nc.gpsimd.tensor_scalar_max(out=safe[:], in0=vpe[:], scalar1=EPS)
+            rstd = small_pool.tile([P, 1], F32, name="rstd")
+            nc.gpsimd.tensor_tensor(out=rstd[:], in0=safe[:], in1=minus_half[:], op=ALU.pow)
+            scale = small_pool.tile([P, 1], F32, name="scale")
+            nc.gpsimd.tensor_tensor(out=scale[:], in0=rstd[:], in1=gain[:, row : row + 1], op=ALU.mult)
+            offset = small_pool.tile([P, 1], F32, name="offset")
+            nc.gpsimd.tensor_scalar(
+                out=offset[:],
+                in0=neg[:, 0:1],
+                scalar1=scale[:],
+                scalar2=shift[:, row : row + 1],
+                op0=ALU.mult,
+                op1=ALU.add,
+            )
+            return scale, offset
+
+        def normalise(j):
+            if j not in range(N):
+                return
+            scale, offset = coeffs[j]
+            nc.scalar.activation(out=msgs[j][:], in_=msgs[j][:], func=ACT.Relu, scale=scale[:], bias=offset[:])
+
+        def finish_edge(j):
+            if j not in range(N):
+                return
+            nc.vector.tensor_tensor(out=msgs[j][:], in0=msgs[j][:], in1=edge_tiles[j][:], op=ALU.add)
+            for half in range(HALVES):
+                nc.sync.dma_start(out=out1_v[half, :, :, j * C : (j + 1) * C], in_=msgs[j][:, half, :])
+            gate = work_pool.tile([P, HALVES, C], F32, name="gate")
+            nc.scalar.activation(out=gate[:], in_=msgs[j][:], func=ACT.Tanh, scale=0.5)
+            gates[j] = den if j == 0 else gate
+            nc.scalar.activation(out=gates[j][:], in_=gate[:], func=ACT.Exp, scale=0.5)
+
+        def fill_value_bank(q):
+            if q not in range(N * QUARTERS):
+                return
+            j, k = divmod(q, QUARTERS)
+            acc = vv_pool.tile([P, BANK], F32, name="vrep")
+            mx_passes(acc, block_of(xr[:, j, :], xrs[:, j, :], k // 2), wv, columns(k), True, True)
+            values[q] = acc
+
+        def add_to_denominator(j):
+            if j not in range(1, N):
+                return
+            nc.vector.tensor_tensor(out=den[:], in0=den[:], in1=gates[j][:], op=ALU.add)
+
+        def weigh_values(j, k):
+            if j not in range(N):
+                return
+            dst = num if j == 0 else gates[j]
+            nc.vector.tensor_tensor(
+                out=dst[:, k // 2, columns(k)],
+                in0=values[QUARTERS * j + k][:],
+                in1=gates[j][:, k // 2, columns(k)],
+                op=ALU.mult,
+            )
+
+        def add_to_numerator(j, half):
+            if j not in range(1, N):
+                return
+            nc.vector.tensor_tensor(out=num[:, half, :], in0=num[:, half, :], in1=gates[j][:, half, :], op=ALU.add)
+
+        for t in range(-2, N + 2):
+            if t >= 0:
+                load_edge(t + PREFETCH)
+            repeat_nodes(t + 2)
+            normalise(t - 1)
+            for k in range(QUARTERS):
+                evacuate(t, k)
+                fill_message_bank(QUARTERS * t + k + MM_BANKS)
+            if t in range(N):
+                square_sum(msgs[t], t)
+            finish_edge(t - 1)
+            transpose_edge(t + 2)
+            if t in range(N):
+                sums = stat_sums(t)
+            add_to_denominator(t - 2)
+            if t in range(N):
+                coeffs[t] = coefficients(sums, t)
+            for k in range(QUARTERS):
+                weigh_values(t - 2, k)
+                fill_value_bank(QUARTERS * (t - 2) + k + VV_BANKS)
+                if k % 2 == 1:
+                    add_to_numerator(t - 2, k // 2)
+            quantise_edge(t + 2)
+
+        nc.scalar.activation(out=den[:], in_=den[:], func=ACT.Abs_reciprocal_sqrt, scale=float(N))
+        nc.scalar.activation(out=den[:], in_=den[:], func=ACT.Square)
+        nc.vector.tensor_tensor(out=num[:], in0=num[:], in1=den[:], op=ALU.mult)
+        y = work_pool.tile([P, HALVES, C], F32, name="msg")
+        for k in range(QUARTERS):
+            acc = mm_pool.tile([P, BANK], F32, name="acc")
+            mx_passes(acc, block_of(xq, xs, k // 2), wu, columns(k), True, True)
+            nc.vector.scalar_tensor_tensor(
+                out=y[:, k // 2, columns(k)],
+                in0=acc[:],
+                scalar=1.0,
+                in1=num[:, k // 2, columns(k)],
+                op0=ALU.mult,
+                op1=ALU.add,
+                accum_out=stats[:, N, k : k + 1],
+            )
+        square_sum(y, N)
+        scale, offset = coefficients(stat_sums(N), N)
+        act = work_pool.tile([P, HALVES, C], F32, name="gate")
+        nc.scalar.activation(out=act[:], in_=y[:], func=ACT.Relu, scale=scale[:], bias=offset[:])
+        nc.vector.tensor_tensor(out=y[:], in0=y[:], in1=act[:], op=ALU.add)
+        for half in range(HALVES):
+            nc.sync.dma_start(out=out0_v[half], in_=y[:, half, :])

@@ -58,13 +58,14 @@ def tile_gnn_s2_pa_t_kernel(
     out0_v = out_0.rearrange("(h l) i c -> h i l c", l=BL)
 
     with ExitStack() as ctx:
-        ctx.enter_context(tc.manual_schedule())
         keep = ctx.enter_context(tc.tile_pool(name="keep", bufs=1))
         edge_pool = ctx.enter_context(tc.tile_pool(name="edge", bufs=PREFETCH + 2))
         group_pool = ctx.enter_context(tc.tile_pool(name="group", bufs=2))
         code_pool = ctx.enter_context(tc.tile_pool(name="code", bufs=3))
-        work_pool = ctx.enter_context(tc.tile_pool(name="work", bufs=3))
-        junk_pool = ctx.enter_context(tc.tile_pool(name="junk", bufs=2))
+        msg_pool = ctx.enter_context(tc.tile_pool(name="msg", bufs=3))
+        gate_pool = ctx.enter_context(tc.tile_pool(name="gate", bufs=2))
+        term_pool = ctx.enter_context(tc.tile_pool(name="term", bufs=2))
+        junk_pool = ctx.enter_context(tc.tile_pool(name="junk", bufs=1))
         small_pool = ctx.enter_context(tc.tile_pool(name="small", bufs=3))
         tp_pool = ctx.enter_context(tc.psum_pool(name="tp", bufs=2))
         mm_pool = ctx.enter_context(tc.psum_pool(name="mm", bufs=MM_BANKS))
@@ -200,6 +201,14 @@ def tile_gnn_s2_pa_t_kernel(
         def columns(k):
             return slice((k % 2) * BANK, (k % 2 + 1) * BANK)
 
+        def flat(t):
+            return t[:].rearrange("p h c -> p (h c)")
+
+        def pieces(j):
+            count = QUARTERS if j == N - 1 else 1
+            width = HALVES * C // count
+            return [slice(i * width, (i + 1) * width) for i in range(count)]
+
         ax = keep.tile([P, HALVES, C], F32, name="ax")
         for k in range(QUARTERS):
             acc = mm_pool.tile([P, BANK], F32, name="acc")
@@ -212,6 +221,7 @@ def tile_gnn_s2_pa_t_kernel(
         values = {}
         msgs = {}
         gates = {}
+        terms = {}
         coeffs = {}
         den = keep.tile([P, HALVES, C], F32, name="den")
         num = keep.tile([P, HALVES, C], F32, name="num")
@@ -248,7 +258,7 @@ def tile_gnn_s2_pa_t_kernel(
             if j not in range(N):
                 return
             if k == 0:
-                msgs[j] = work_pool.tile([P, HALVES, C], F32, name="msg")
+                msgs[j] = msg_pool.tile([P, HALVES, C], F32, name="msg")
             nc.vector.scalar_tensor_tensor(
                 out=msgs[j][:, k // 2, columns(k)],
                 in0=banks[QUARTERS * j + k][:],
@@ -259,9 +269,15 @@ def tile_gnn_s2_pa_t_kernel(
                 accum_out=stats[:, j, k : k + 1],
             )
 
-        def square_sum(values_tile, row):
+        def square_sum(values_tile, row, ranges):
             junk = junk_pool.tile([P, HALVES, C], BF16, name="junk")
-            nc.scalar.activation(out=junk[:], in_=values_tile[:], func=ACT.Square, accum_out=stats[:, row, 8:9])
+            for index, cols in enumerate(ranges):
+                nc.scalar.activation(
+                    out=flat(junk)[:, cols],
+                    in_=flat(values_tile)[:, cols],
+                    func=ACT.Square,
+                    accum_out=stats[:, row, 8 + index : 9 + index],
+                )
 
         def stat_sums(row):
             sums = sp_pool.tile([P, 16], F32, name="sums")
@@ -300,18 +316,35 @@ def tile_gnn_s2_pa_t_kernel(
             if j not in range(N):
                 return
             scale, offset = coeffs[j]
-            nc.scalar.activation(out=msgs[j][:], in_=msgs[j][:], func=ACT.Relu, scale=scale[:], bias=offset[:])
+            for cols in pieces(j):
+                nc.scalar.activation(
+                    out=flat(msgs[j])[:, cols], in_=flat(msgs[j])[:, cols], func=ACT.Relu, scale=scale[:], bias=offset[:]
+                )
 
         def finish_edge(j):
             if j not in range(N):
                 return
-            nc.vector.tensor_tensor(out=msgs[j][:], in0=msgs[j][:], in1=edge_tiles[j][:], op=ALU.add)
+            for cols in pieces(j):
+                nc.vector.tensor_tensor(
+                    out=flat(msgs[j])[:, cols], in0=flat(msgs[j])[:, cols], in1=flat(edge_tiles[j])[:, cols], op=ALU.add
+                )
             for half in range(HALVES):
                 nc.sync.dma_start(out=out1_v[half, :, :, j * C : (j + 1) * C], in_=msgs[j][:, half, :])
-            gate = work_pool.tile([P, HALVES, C], F32, name="gate")
-            nc.scalar.activation(out=gate[:], in_=msgs[j][:], func=ACT.Tanh, scale=0.5)
-            gates[j] = den if j == 0 else gate
-            nc.scalar.activation(out=gates[j][:], in_=gate[:], func=ACT.Exp, scale=0.5)
+            gate = gate_pool.tile([P, HALVES, C], F32, name="gate")
+            for cols in pieces(j):
+                nc.scalar.activation(out=flat(gate)[:, cols], in_=flat(msgs[j])[:, cols], func=ACT.Tanh, scale=0.5)
+            for cols in pieces(j):
+                nc.scalar.activation(out=flat(gate)[:, cols], in_=flat(gate)[:, cols], func=ACT.Exp, scale=0.5)
+            gates[j] = gate
+            if j > 0:
+                so_far = gates[0] if j == 1 else den
+                for k in range(QUARTERS):
+                    nc.gpsimd.tensor_tensor(
+                        out=den[:, k // 2, columns(k)],
+                        in0=so_far[:, k // 2, columns(k)],
+                        in1=gate[:, k // 2, columns(k)],
+                        op=ALU.add,
+                    )
 
         def fill_value_bank(q):
             if q not in range(N * QUARTERS):
@@ -321,17 +354,13 @@ def tile_gnn_s2_pa_t_kernel(
             mx_passes(acc, block_of(xr[:, j, :], xrs[:, j, :], k // 2), wv, columns(k), True, True)
             values[q] = acc
 
-        def add_to_denominator(j):
-            if j not in range(1, N):
-                return
-            nc.vector.tensor_tensor(out=den[:], in0=den[:], in1=gates[j][:], op=ALU.add)
-
         def weigh_values(j, k):
             if j not in range(N):
                 return
-            dst = num if j == 0 else gates[j]
+            if k == 0:
+                terms[j] = num if j == 0 else term_pool.tile([P, HALVES, C], F32, name="term")
             nc.vector.tensor_tensor(
-                out=dst[:, k // 2, columns(k)],
+                out=terms[j][:, k // 2, columns(k)],
                 in0=values[QUARTERS * j + k][:],
                 in1=gates[j][:, k // 2, columns(k)],
                 op=ALU.mult,
@@ -340,7 +369,7 @@ def tile_gnn_s2_pa_t_kernel(
         def add_to_numerator(j, half):
             if j not in range(1, N):
                 return
-            nc.vector.tensor_tensor(out=num[:, half, :], in0=num[:, half, :], in1=gates[j][:, half, :], op=ALU.add)
+            nc.vector.tensor_tensor(out=num[:, half, :], in0=num[:, half, :], in1=terms[j][:, half, :], op=ALU.add)
 
         for t in range(-2, N + 2):
             if t >= 0:
@@ -351,12 +380,11 @@ def tile_gnn_s2_pa_t_kernel(
                 evacuate(t, k)
                 fill_message_bank(QUARTERS * t + k + MM_BANKS)
             if t in range(N):
-                square_sum(msgs[t], t)
+                square_sum(msgs[t], t, pieces(t))
             finish_edge(t - 1)
             transpose_edge(t + 2)
             if t in range(N):
                 sums = stat_sums(t)
-            add_to_denominator(t - 2)
             if t in range(N):
                 coeffs[t] = coefficients(sums, t)
             for k in range(QUARTERS):
@@ -366,26 +394,29 @@ def tile_gnn_s2_pa_t_kernel(
                     add_to_numerator(t - 2, k // 2)
             quantise_edge(t + 2)
 
-        nc.scalar.activation(out=den[:], in_=den[:], func=ACT.Abs_reciprocal_sqrt, scale=float(N))
-        nc.scalar.activation(out=den[:], in_=den[:], func=ACT.Square)
-        nc.vector.tensor_tensor(out=num[:], in0=num[:], in1=den[:], op=ALU.mult)
-        y = work_pool.tile([P, HALVES, C], F32, name="msg")
+        y = msg_pool.tile([P, HALVES, C], F32, name="msg")
         for k in range(QUARTERS):
+            part = (slice(None), k // 2, columns(k))
+            nc.scalar.activation(out=den[part], in_=den[part], func=ACT.Abs_reciprocal_sqrt, scale=float(N))
+            nc.scalar.activation(out=den[part], in_=den[part], func=ACT.Square)
+            nc.vector.tensor_tensor(out=num[part], in0=num[part], in1=den[part], op=ALU.mult)
             acc = mm_pool.tile([P, BANK], F32, name="acc")
             mx_passes(acc, block_of(xq, xs, k // 2), wu, columns(k), True, True)
             nc.vector.scalar_tensor_tensor(
-                out=y[:, k // 2, columns(k)],
+                out=y[part],
                 in0=acc[:],
                 scalar=1.0,
-                in1=num[:, k // 2, columns(k)],
+                in1=num[part],
                 op0=ALU.mult,
                 op1=ALU.add,
                 accum_out=stats[:, N, k : k + 1],
             )
-        square_sum(y, N)
+        square_sum(y, N, pieces(N - 1))
         scale, offset = coefficients(stat_sums(N), N)
-        act = work_pool.tile([P, HALVES, C], F32, name="gate")
-        nc.scalar.activation(out=act[:], in_=y[:], func=ACT.Relu, scale=scale[:], bias=offset[:])
-        nc.vector.tensor_tensor(out=y[:], in0=y[:], in1=act[:], op=ALU.add)
-        for half in range(HALVES):
-            nc.sync.dma_start(out=out0_v[half], in_=y[:, half, :])
+        act = gate_pool.tile([P, HALVES, C], F32, name="gate")
+        for k in range(QUARTERS):
+            part = (slice(None), k // 2, columns(k))
+            nc.scalar.activation(out=act[part], in_=y[part], func=ACT.Relu, scale=scale[:], bias=offset[:])
+            nc.vector.tensor_tensor(out=y[part], in0=y[part], in1=act[part], op=ALU.add)
+            if k % 2 == 1:
+                nc.sync.dma_start(out=out0_v[k // 2], in_=y[:, k // 2, :])

@@ -338,12 +338,9 @@ def tile_gnn_s2_pa_t_kernel(
             gates[j] = gate
             if j > 0:
                 so_far = gates[0] if j == 1 else den
-                for k in range(QUARTERS):
-                    nc.gpsimd.tensor_tensor(
-                        out=den[:, k // 2, columns(k)],
-                        in0=so_far[:, k // 2, columns(k)],
-                        in1=gate[:, k // 2, columns(k)],
-                        op=ALU.add,
+                for cols in pieces(j):
+                    nc.vector.tensor_tensor(
+                        out=flat(den)[:, cols], in0=flat(so_far)[:, cols], in1=flat(gate)[:, cols], op=ALU.add
                     )
 
         def fill_value_bank(q):

@@ -58,6 +58,7 @@ def tile_gnn_s2_pa_t_kernel(
     out0_v = out_0.rearrange("(h l) i c -> h i l c", l=BL)
 
     with ExitStack() as ctx:
+        ctx.enter_context(tc.manual_schedule())
         keep = ctx.enter_context(tc.tile_pool(name="keep", bufs=1))
         edge_pool = ctx.enter_context(tc.tile_pool(name="edge", bufs=PREFETCH + 2))
         group_pool = ctx.enter_context(tc.tile_pool(name="group", bufs=2))
@@ -94,6 +95,22 @@ def tile_gnn_s2_pa_t_kernel(
                 nc.sync.dma_start(out=et[:, half, :], in_=edge_v[half, :, :, j * C : (j + 1) * C])
             edge_tiles[j] = et
 
+        params = []
+        for by_edge, by_node, label in ((bne_w, bnv_w, "w"), (bne_b, bnv_b, "b")):
+            e_bf = keep.tile([P, N], BF16, name="bne_" + label)
+            v_bf = keep.tile([P, 1], BF16, name="bnv_" + label)
+            nc.scalar.dma_start(
+                out=e_bf[:], in_=by_edge.rearrange("(i j) -> i j", j=N).unsqueeze(1).to_broadcast([N, BL, N])
+            )
+            nc.scalar.dma_start(
+                out=v_bf[:], in_=by_node.rearrange("(i o) -> i o", o=1).unsqueeze(1).to_broadcast([N, BL, 1])
+            )
+            params.append((e_bf, v_bf))
+
+        warm = keep.tile([P, 1], F32, name="warm")
+        nc.vector.memset(warm[:], 0.0)
+        nc.scalar.activation(out=warm[:], in_=warm[:], func=ACT.Tanh)
+
         x_sb = keep.tile([P, HALVES, C], BF16, name="x_sb")
         nc.sync.dma_start(out=x_sb[:], in_=x.rearrange("(h l) n c -> (l n) h c", l=BL))
         wa = load_weight(Wa_words, Wa_scales, "wa")
@@ -104,24 +121,6 @@ def tile_gnn_s2_pa_t_kernel(
             load_edge(j)
         wv = load_weight(Wv_words, Wv_scales, "wv")
         wu = load_weight(Wu_words, Wu_scales, "wu")
-
-        gain = keep.tile([P, N + 1], F32, name="gain")
-        shift = keep.tile([P, N + 1], F32, name="shift")
-        for dst, by_edge, by_node, label in ((gain, bne_w, bnv_w, "w"), (shift, bne_b, bnv_b, "b")):
-            e_bf = keep.tile([P, N], BF16, name="bne_" + label)
-            v_bf = keep.tile([P, 1], BF16, name="bnv_" + label)
-            nc.scalar.dma_start(
-                out=e_bf[:], in_=by_edge.rearrange("(i j) -> i j", j=N).unsqueeze(1).to_broadcast([N, BL, N])
-            )
-            nc.scalar.dma_start(
-                out=v_bf[:], in_=by_node.rearrange("(i o) -> i o", o=1).unsqueeze(1).to_broadcast([N, BL, 1])
-            )
-            nc.vector.tensor_copy(out=dst[:, 0:N], in_=e_bf[:])
-            nc.vector.tensor_copy(out=dst[:, N : N + 1], in_=v_bf[:])
-
-        warm = keep.tile([P, 1], F32, name="warm")
-        nc.vector.memset(warm[:], 0.0)
-        nc.scalar.activation(out=warm[:], in_=warm[:], func=ACT.Tanh)
 
         ident = keep.tile([P, P], F32, name="ident")
         make_identity(nc, ident[:])
@@ -159,6 +158,12 @@ def tile_gnn_s2_pa_t_kernel(
         xs = keep.tile([P, G * HALVES * P], U8, name="xs", align_bytes=64)
         nc.vector.memset(xs[:].bitcast(I32), 0)
         nc.vector.quantize_mx(out=xq[:].bitcast(FP8X4), scales=xs[:], in_=xg[:])
+
+        gain = keep.tile([P, N + 1], F32, name="gain")
+        shift = keep.tile([P, N + 1], F32, name="shift")
+        for dst, (e_bf, v_bf) in zip((gain, shift), params):
+            nc.vector.tensor_copy(out=dst[:, 0:N], in_=e_bf[:])
+            nc.vector.tensor_copy(out=dst[:, N : N + 1], in_=v_bf[:])
 
         xr = keep.tile([P, N, G * HALVES * P], I32, name="xr", align_bytes=64)
         xrs = keep.tile([P, N, G * HALVES * P], U8, name="xrs", align_bytes=64)
@@ -215,6 +220,7 @@ def tile_gnn_s2_pa_t_kernel(
             mx_passes(acc, block_of(xq, xs, k // 2), wa, columns(k), True, True)
             nc.scalar.copy(out=ax[:, k // 2, columns(k)], in_=acc[:])
 
+        flipped = {}
         groups = {}
         codes = {}
         banks = {}
@@ -229,12 +235,18 @@ def tile_gnn_s2_pa_t_kernel(
         def transpose_edge(j):
             if j not in range(N):
                 return
-            eg = group_pool.tile([P, G * HALVES * P * 4], BF16, name="eg", align_bytes=64)
-            eg_words = eg[:].bitcast(F32).rearrange("p (g h r u) -> p g h r u", g=G, h=HALVES, u=2)
             for half in range(HALVES):
                 bank = tp_pool.tile([P, G, 2, P], F32, name="bank")
                 transpose_words(bank, edge_tiles[j][:, half, :])
-                nc.scalar.copy(out=eg_words[:, :, half], in_=bank[:].rearrange("p g u r -> p g r u"))
+                flipped[j, half] = bank
+
+        def group_edge(j):
+            if j not in range(N):
+                return
+            eg = group_pool.tile([P, G * HALVES * P * 4], BF16, name="eg", align_bytes=64)
+            eg_words = eg[:].bitcast(F32).rearrange("p (g h r u) -> p g h r u", g=G, h=HALVES, u=2)
+            for half in range(HALVES):
+                nc.scalar.copy(out=eg_words[:, :, half], in_=flipped[j, half][:].rearrange("p g u r -> p g r u"))
             groups[j] = eg
 
         def quantise_edge(j):
@@ -333,15 +345,9 @@ def tile_gnn_s2_pa_t_kernel(
             gate = gate_pool.tile([P, HALVES, C], F32, name="gate")
             for cols in pieces(j):
                 nc.scalar.activation(out=flat(gate)[:, cols], in_=flat(msgs[j])[:, cols], func=ACT.Tanh, scale=0.5)
+            gates[j] = den if j == 0 else gate
             for cols in pieces(j):
-                nc.scalar.activation(out=flat(gate)[:, cols], in_=flat(gate)[:, cols], func=ACT.Exp, scale=0.5)
-            gates[j] = gate
-            if j > 0:
-                so_far = gates[0] if j == 1 else den
-                for cols in pieces(j):
-                    nc.vector.tensor_tensor(
-                        out=flat(den)[:, cols], in0=flat(so_far)[:, cols], in1=flat(gate)[:, cols], op=ALU.add
-                    )
+                nc.scalar.activation(out=flat(gates[j])[:, cols], in_=flat(gate)[:, cols], func=ACT.Exp, scale=0.5)
 
         def fill_value_bank(q):
             if q not in range(N * QUARTERS):
@@ -350,6 +356,14 @@ def tile_gnn_s2_pa_t_kernel(
             acc = vv_pool.tile([P, BANK], F32, name="vrep")
             mx_passes(acc, block_of(xr[:, j, :], xrs[:, j, :], k // 2), wv, columns(k), True, True)
             values[q] = acc
+
+        def add_to_denominator(j):
+            if j not in range(1, N):
+                return
+            for cols in pieces(j):
+                nc.vector.tensor_tensor(
+                    out=flat(den)[:, cols], in0=flat(den)[:, cols], in1=flat(gates[j])[:, cols], op=ALU.add
+                )
 
         def weigh_values(j, k):
             if j not in range(N):
@@ -368,28 +382,31 @@ def tile_gnn_s2_pa_t_kernel(
                 return
             nc.vector.tensor_tensor(out=num[:, half, :], in0=num[:, half, :], in1=terms[j][:, half, :], op=ALU.add)
 
-        for t in range(-2, N + 2):
+        for t in range(-3, N + 2):
             if t >= 0:
                 load_edge(t + PREFETCH)
-            repeat_nodes(t + 2)
+            repeat_nodes(t + 3)
             normalise(t - 1)
+            group_edge(t + 2)
             for k in range(QUARTERS):
+                if k == 2:
+                    add_to_denominator(t - 2)
                 evacuate(t, k)
                 fill_message_bank(QUARTERS * t + k + MM_BANKS)
             if t in range(N):
                 square_sum(msgs[t], t, pieces(t))
             finish_edge(t - 1)
-            transpose_edge(t + 2)
             if t in range(N):
                 sums = stat_sums(t)
-            if t in range(N):
-                coeffs[t] = coefficients(sums, t)
             for k in range(QUARTERS):
                 weigh_values(t - 2, k)
                 fill_value_bank(QUARTERS * (t - 2) + k + VV_BANKS)
+                if k == 1 and t in range(N):
+                    coeffs[t] = coefficients(sums, t)
                 if k % 2 == 1:
                     add_to_numerator(t - 2, k // 2)
             quantise_edge(t + 2)
+            transpose_edge(t + 3)
 
         y = msg_pool.tile([P, HALVES, C], F32, name="msg")
         for k in range(QUARTERS):

@@ -134,7 +134,7 @@ def tile_gnn_s2_pa_t_kernel(
         )
         minus_half = keep.tile([P, 1], F32, name="minus_half")
         nc.vector.memset(minus_half[:], -0.5)
-        stats = keep.tile([P, N + 1, 16], F32, name="stats")
+        stats = keep.tile([P, N + 1, 32], F32, name="stats")
         nc.vector.memset(stats[:], 0.0)
 
         def transpose_words(bank, rows):
@@ -214,11 +214,11 @@ def tile_gnn_s2_pa_t_kernel(
             width = HALVES * C // count
             return [slice(i * width, (i + 1) * width) for i in range(count)]
 
-        ax = keep.tile([P, HALVES, C], F32, name="ax")
-        for k in range(QUARTERS):
+        ax = keep.tile([P, C], F32, name="ax")
+        for k in range(QUARTERS // 2):
             acc = mm_pool.tile([P, BANK], F32, name="acc")
-            mx_passes(acc, block_of(xq, xs, k // 2), wa, columns(k), True, True)
-            nc.scalar.copy(out=ax[:, k // 2, columns(k)], in_=acc[:])
+            mx_passes(acc, block_of(xq, xs, 0), wa, columns(k), True, True)
+            nc.scalar.copy(out=ax[:, columns(k)], in_=acc[:])
 
         flipped = {}
         groups = {}
@@ -263,6 +263,8 @@ def tile_gnn_s2_pa_t_kernel(
             j, k = divmod(q, QUARTERS)
             acc = mm_pool.tile([P, BANK], F32, name="acc")
             mx_passes(acc, block_of(codes[j][0], codes[j][1], k // 2), we, columns(k), True, False)
+            if k // 2 == 1:
+                mx_passes(acc, block_of(xq, xs, 1), wa, columns(k), False, False)
             mx_passes(acc, block_of(xr[:, j, :], xrs[:, j, :], k // 2), wb, columns(k), False, True)
             banks[q] = acc
 
@@ -271,15 +273,23 @@ def tile_gnn_s2_pa_t_kernel(
                 return
             if k == 0:
                 msgs[j] = msg_pool.tile([P, HALVES, C], F32, name="msg")
-            nc.vector.scalar_tensor_tensor(
-                out=msgs[j][:, k // 2, columns(k)],
-                in0=banks[QUARTERS * j + k][:],
-                scalar=1.0,
-                in1=ax[:, k // 2, columns(k)],
-                op0=ALU.mult,
-                op1=ALU.add,
-                accum_out=stats[:, j, k : k + 1],
-            )
+            if k // 2 == 0:
+                nc.vector.scalar_tensor_tensor(
+                    out=msgs[j][:, 0, columns(k)],
+                    in0=banks[QUARTERS * j + k][:],
+                    scalar=1.0,
+                    in1=ax[:, columns(k)],
+                    op0=ALU.mult,
+                    op1=ALU.add,
+                    accum_out=stats[:, j, k : k + 1],
+                )
+            else:
+                nc.scalar.activation(
+                    out=msgs[j][:, 1, columns(k)],
+                    in_=banks[QUARTERS * j + k][:],
+                    func=ACT.Identity,
+                    accum_out=stats[:, j, 8 + k % 2 : 9 + k % 2],
+                )
 
         def square_sum(values_tile, row, ranges):
             junk = junk_pool.tile([P, HALVES, C], BF16, name="junk")
@@ -288,11 +298,11 @@ def tile_gnn_s2_pa_t_kernel(
                     out=flat(junk)[:, cols],
                     in_=flat(values_tile)[:, cols],
                     func=ACT.Square,
-                    accum_out=stats[:, row, 8 + index : 9 + index],
+                    accum_out=stats[:, row, 16 + index : 17 + index],
                 )
 
         def stat_sums(row):
-            sums = sp_pool.tile([P, 16], F32, name="sums")
+            sums = sp_pool.tile([P, 32], F32, name="sums")
             nc.tensor.matmul(
                 out=sums[:], lhsT=group_mean[:].rearrange("p i l -> p (i l)"), rhs=stats[:, row, :], start=True, stop=True
             )
@@ -387,25 +397,25 @@ def tile_gnn_s2_pa_t_kernel(
                 load_edge(t + PREFETCH)
             repeat_nodes(t + 3)
             normalise(t - 1)
-            group_edge(t + 2)
             for k in range(QUARTERS):
-                if k == 2:
-                    add_to_denominator(t - 2)
                 evacuate(t, k)
                 fill_message_bank(QUARTERS * t + k + MM_BANKS)
             if t in range(N):
                 square_sum(msgs[t], t, pieces(t))
+            group_edge(t + 2)
+            add_to_denominator(t - 2)
             finish_edge(t - 1)
             if t in range(N):
                 sums = stat_sums(t)
             for k in range(QUARTERS):
                 weigh_values(t - 2, k)
                 fill_value_bank(QUARTERS * (t - 2) + k + VV_BANKS)
-                if k == 1 and t in range(N):
-                    coeffs[t] = coefficients(sums, t)
-                if k % 2 == 1:
-                    add_to_numerator(t - 2, k // 2)
+                if k == 1:
+                    add_to_numerator(t - 2, 0)
+            if t in range(N):
+                coeffs[t] = coefficients(sums, t)
             quantise_edge(t + 2)
+            add_to_numerator(t - 2, 1)
             transpose_edge(t + 3)
 
         y = msg_pool.tile([P, HALVES, C], F32, name="msg")
@@ -432,5 +442,4 @@ def tile_gnn_s2_pa_t_kernel(
             part = (slice(None), k // 2, columns(k))
             nc.scalar.activation(out=act[part], in_=y[part], func=ACT.Relu, scale=scale[:], bias=offset[:])
             nc.vector.tensor_tensor(out=y[part], in0=y[part], in1=act[part], op=ALU.add)
-            if k % 2 == 1:
-                nc.sync.dma_start(out=out0_v[k // 2], in_=y[:, k // 2, :])
+            nc.sync.dma_start(out=out0_v[k // 2, :, :, columns(k)], in_=y[part])

@@ -60,12 +60,12 @@ def tile_gnn_s2_pa_t_kernel(
     with ExitStack() as ctx:
         ctx.enter_context(tc.manual_schedule())
         keep = ctx.enter_context(tc.tile_pool(name="keep", bufs=1))
-        edge_pool = ctx.enter_context(tc.tile_pool(name="edge", bufs=PREFETCH + 2))
+        edge_pool = ctx.enter_context(tc.tile_pool(name="edge", bufs=PREFETCH + 3))
         group_pool = ctx.enter_context(tc.tile_pool(name="group", bufs=2))
         code_pool = ctx.enter_context(tc.tile_pool(name="code", bufs=3))
-        msg_pool = ctx.enter_context(tc.tile_pool(name="msg", bufs=3))
+        msg_pool = ctx.enter_context(tc.tile_pool(name="msg", bufs=4))
         gate_pool = ctx.enter_context(tc.tile_pool(name="gate", bufs=2))
-        term_pool = ctx.enter_context(tc.tile_pool(name="term", bufs=2))
+        term_pool = ctx.enter_context(tc.tile_pool(name="term", bufs=1))
         junk_pool = ctx.enter_context(tc.tile_pool(name="junk", bufs=1))
         small_pool = ctx.enter_context(tc.tile_pool(name="small", bufs=3))
         tp_pool = ctx.enter_context(tc.psum_pool(name="tp", bufs=2))
@@ -392,30 +392,30 @@ def tile_gnn_s2_pa_t_kernel(
                 return
             nc.vector.tensor_tensor(out=num[:, half, :], in0=num[:, half, :], in1=terms[j][:, half, :], op=ALU.add)
 
-        for t in range(-3, N + 2):
+        for t in range(-3, N + 3):
             if t >= 0:
                 load_edge(t + PREFETCH)
             repeat_nodes(t + 3)
-            normalise(t - 1)
+            normalise(t - 2)
             for k in range(QUARTERS):
                 evacuate(t, k)
                 fill_message_bank(QUARTERS * t + k + MM_BANKS)
             if t in range(N):
                 square_sum(msgs[t], t, pieces(t))
             group_edge(t + 2)
-            add_to_denominator(t - 2)
-            finish_edge(t - 1)
+            add_to_denominator(t - 3)
+            finish_edge(t - 2)
             if t in range(N):
                 sums = stat_sums(t)
             for k in range(QUARTERS):
-                weigh_values(t - 2, k)
-                fill_value_bank(QUARTERS * (t - 2) + k + VV_BANKS)
+                weigh_values(t - 3, k)
+                fill_value_bank(QUARTERS * (t - 3) + k + VV_BANKS)
                 if k == 1:
-                    add_to_numerator(t - 2, 0)
-            if t in range(N):
-                coeffs[t] = coefficients(sums, t)
+                    if t in range(N):
+                        coeffs[t] = coefficients(sums, t)
+                    add_to_numerator(t - 3, 0)
             quantise_edge(t + 2)
-            add_to_numerator(t - 2, 1)
+            add_to_numerator(t - 3, 1)
             transpose_edge(t + 3)
 
         y = msg_pool.tile([P, HALVES, C], F32, name="msg")

@@ -26,7 +26,7 @@ COUNT = 16 * C
 MM_BANKS = 3
 VV_BANKS = 2
 PREFETCH = 4
-REP = 8
+REP = 4
 
 FLOPS = 2 * C * C * (16 * 256 + 4 * 16 * 16)
 
@@ -53,9 +53,9 @@ def tile_gnn_s2_pa_t_kernel(
     out_1,
 ):
     nc = tc.nc
-    edge_v = edge.rearrange("(h l) (i j) c -> h i l (j c)", l=BL, j=N)
-    out1_v = out_1.rearrange("(h l) (i j) c -> h i l (j c)", l=BL, j=N)
-    out0_v = out_0.rearrange("(h l) i c -> h i l c", l=BL)
+    edge_v = edge.rearrange("(h l) (i j) c -> h (l i) (j c)", l=BL, j=N)
+    out1_v = out_1.rearrange("(h l) (i j) c -> h (l i) (j c)", l=BL, j=N)
+    out0_v = out_0.rearrange("(h l) i c -> h (l i) c", l=BL)
 
     with ExitStack() as ctx:
         ctx.enter_context(tc.manual_schedule())
@@ -92,7 +92,7 @@ def tile_gnn_s2_pa_t_kernel(
                 return
             et = edge_pool.tile([P, HALVES, C], BF16, name="et")
             for half in range(HALVES):
-                nc.sync.dma_start(out=et[:, half, :], in_=edge_v[half, :, :, j * C : (j + 1) * C])
+                nc.sync.dma_start(out=et[:, half, :], in_=edge_v[half, :, j * C : (j + 1) * C])
             edge_tiles[j] = et
 
         params = []
@@ -100,10 +100,10 @@ def tile_gnn_s2_pa_t_kernel(
             e_bf = keep.tile([P, N], BF16, name="bne_" + label)
             v_bf = keep.tile([P, 1], BF16, name="bnv_" + label)
             nc.scalar.dma_start(
-                out=e_bf[:], in_=by_edge.rearrange("(i j) -> i j", j=N).unsqueeze(1).to_broadcast([N, BL, N])
+                out=e_bf[:], in_=by_edge.rearrange("(i j) -> i j", j=N).unsqueeze(0).to_broadcast([BL, N, N])
             )
             nc.scalar.dma_start(
-                out=v_bf[:], in_=by_node.rearrange("(i o) -> i o", o=1).unsqueeze(1).to_broadcast([N, BL, 1])
+                out=v_bf[:], in_=by_node.rearrange("(i o) -> i o", o=1).unsqueeze(0).to_broadcast([BL, N, 1])
             )
             params.append((e_bf, v_bf))
 
@@ -126,11 +126,11 @@ def tile_gnn_s2_pa_t_kernel(
         make_identity(nc, ident[:])
         same_i = keep.tile([P, N], F32, name="same_i")
         nc.vector.tensor_reduce(
-            out=same_i[:], in_=ident[:].rearrange("p (i l) -> p i l", l=BL), axis=AX.X, op=ALU.add
+            out=same_i[:], in_=ident[:].rearrange("p (l i) -> p i l", l=BL), axis=AX.X, op=ALU.add
         )
-        group_mean = keep.tile([P, N, BL], F32, name="group_mean")
+        group_mean = keep.tile([P, BL, N], F32, name="group_mean")
         nc.vector.tensor_scalar_mul(
-            out=group_mean[:], in0=same_i[:].unsqueeze(2).to_broadcast([P, N, BL]), scalar1=-1.0 / COUNT
+            out=group_mean[:], in0=same_i[:].unsqueeze(1).to_broadcast([P, BL, N]), scalar1=-1.0 / COUNT
         )
         minus_half = keep.tile([P, 1], F32, name="minus_half")
         nc.vector.memset(minus_half[:], -0.5)
@@ -146,18 +146,28 @@ def tile_gnn_s2_pa_t_kernel(
                     )
 
         xg = keep.tile([P, G * HALVES * P * 4], BF16, name="xg", align_bytes=64)
-        xg_words = xg[:].bitcast(F32).rearrange("p (g h n l u) -> p g h n l u", g=G, h=HALVES, n=N, l=BL)
+        xg_words = xg[:].bitcast(F32).rearrange("p (g h r u) -> p g h r u", g=G, h=HALVES, u=2)
+        xs4 = keep.tile([P, G * HALVES * P * 4], U8, name="xs4", align_bytes=64)
+        nc.vector.memset(xs4[:].bitcast(I32), 0)
+        x_banks = []
         for half in range(HALVES):
             bank = tp_pool.tile([P, G, 2, P], F32, name="bank")
             transpose_words(bank, x_sb[:, half, :])
-            for g in range(G):
-                nc.vector.tensor_copy(
-                    out=xg_words[:, g, half], in_=bank[:, g].rearrange("p u (l n) -> p n l u", l=BL)
-                )
+            nc.vector.tensor_copy(out=xg_words[:, :, half], in_=bank[:].rearrange("p g u r -> p g r u"))
+            x_banks.append(bank)
         xq = keep.tile([P, G * HALVES * P], I32, name="xq", align_bytes=64)
         xs = keep.tile([P, G * HALVES * P], U8, name="xs", align_bytes=64)
-        nc.vector.memset(xs[:].bitcast(I32), 0)
         nc.vector.quantize_mx(out=xq[:].bitcast(FP8X4), scales=xs[:], in_=xg[:])
+        for half in range(HALVES):
+            for g in range(G):
+                eg = group_pool.tile([P, P * 4 * 4], BF16, name="eg", align_bytes=64)
+                nc.scalar.copy(
+                    out=eg[:].bitcast(F32).rearrange("p (r f u) -> p r f u", f=4, u=2),
+                    in_=x_banks[half][:, g].rearrange("p u r -> p r u").unsqueeze(2).to_broadcast([P, P, 4, 2]),
+                )
+                eq = code_pool.tile([P, P * 4], I32, name="eq", align_bytes=64)
+                block = slice((g * HALVES + half) * P * 4, (g * HALVES + half + 1) * P * 4)
+                nc.vector.quantize_mx(out=eq[:].bitcast(FP8X4), scales=xs4[:, block], in_=eg[:])
 
         gain = keep.tile([P, N + 1], F32, name="gain")
         shift = keep.tile([P, N + 1], F32, name="shift")
@@ -167,20 +177,20 @@ def tile_gnn_s2_pa_t_kernel(
 
         xr = keep.tile([P, N, G * HALVES * P], I32, name="xr", align_bytes=64)
         xrs = keep.tile([P, N, G * HALVES * P], U8, name="xrs", align_bytes=64)
-        xq_v = xq[:].rearrange("p (a n l) -> p n a l", a=G * HALVES, n=N)
-        xs_v = xs[:].bitcast(I32).rearrange("p (a n w) -> p n a w", a=G * HALVES, n=N)
+        xq_v = xq[:].rearrange("p (a l n) -> p n a l", a=G * HALVES, l=BL)
+        xs4_v = xs4[:].bitcast(I32).rearrange("p (a l n) -> p n a l", a=G * HALVES, l=BL)
 
         def repeat_nodes(block):
             if block not in range(N // REP):
                 return
             js = slice(block * REP, (block + 1) * REP)
             nc.vector.tensor_copy(
-                out=xr[:, js, :].rearrange("p j (a i l) -> p j a i l", a=G * HALVES, i=N),
-                in_=xq_v[:, js].unsqueeze(3).to_broadcast([P, REP, G * HALVES, N, BL]),
+                out=xr[:, js, :].rearrange("p j (a l i) -> p j a l i", a=G * HALVES, l=BL),
+                in_=xq_v[:, js].unsqueeze(4).to_broadcast([P, REP, G * HALVES, BL, N]),
             )
             nc.vector.tensor_copy(
-                out=xrs[:, js, :].bitcast(I32).rearrange("p j (a i w) -> p j a i w", a=G * HALVES, i=N),
-                in_=xs_v[:, js].unsqueeze(3).to_broadcast([P, REP, G * HALVES, N, 2]),
+                out=xrs[:, js, :].bitcast(I32).rearrange("p j (a l w) -> p j a l w", a=G * HALVES, l=BL),
+                in_=xs4_v[:, js].unsqueeze(4).to_broadcast([P, REP, G * HALVES, BL, 4]),
             )
 
         def mx_passes(acc, stationary, weights, cols, first, last):
@@ -304,7 +314,7 @@ def tile_gnn_s2_pa_t_kernel(
         def stat_sums(row):
             sums = sp_pool.tile([P, 32], F32, name="sums")
             nc.tensor.matmul(
-                out=sums[:], lhsT=group_mean[:].rearrange("p i l -> p (i l)"), rhs=stats[:, row, :], start=True, stop=True
+                out=sums[:], lhsT=group_mean[:].rearrange("p l i -> p (l i)"), rhs=stats[:, row, :], start=True, stop=True
             )
             return sums
 
@@ -351,7 +361,7 @@ def tile_gnn_s2_pa_t_kernel(
                     out=flat(msgs[j])[:, cols], in0=flat(msgs[j])[:, cols], in1=flat(edge_tiles[j])[:, cols], op=ALU.add
                 )
             for half in range(HALVES):
-                nc.sync.dma_start(out=out1_v[half, :, :, j * C : (j + 1) * C], in_=msgs[j][:, half, :])
+                nc.sync.dma_start(out=out1_v[half, :, j * C : (j + 1) * C], in_=msgs[j][:, half, :])
             gate = gate_pool.tile([P, HALVES, C], F32, name="gate")
             for cols in pieces(j):
                 nc.scalar.activation(out=flat(gate)[:, cols], in_=flat(msgs[j])[:, cols], func=ACT.Tanh, scale=0.5)
@@ -442,4 +452,4 @@ def tile_gnn_s2_pa_t_kernel(
             part = (slice(None), k // 2, columns(k))
             nc.scalar.activation(out=act[part], in_=y[part], func=ACT.Relu, scale=scale[:], bias=offset[:])
             nc.vector.tensor_tensor(out=y[part], in0=y[part], in1=act[part], op=ALU.add)
-            nc.sync.dma_start(out=out0_v[k // 2, :, :, columns(k)], in_=y[part])
+            nc.sync.dma_start(out=out0_v[k // 2, :, columns(k)], in_=y[part])

@@ -15,18 +15,19 @@ AX = mybir.AxisListType
 P = 128
 N = 16
 C = 1024
-HALVES = 2
-BL = 8
+H = 2
+Q = 8
+W = H * C
 G = 2
 BANK = 512
-QUARTERS = 4
+QUARTERS = W // BANK
+STEPS = H * Q
+CHUNKS = C // P
 EPS = 1e-5
 COUNT = 16 * C
 
-MM_BANKS = 3
-VV_BANKS = 2
+MM_BANKS = 2
 PREFETCH = 4
-REP = 4
 
 FLOPS = 2 * C * C * (16 * 256 + 4 * 16 * 16)
 
@@ -53,25 +54,25 @@ def tile_gnn_s2_pa_t_kernel(
     out_1,
 ):
     nc = tc.nc
-    edge_v = edge.rearrange("(h l) (i j) c -> h (l i) (j c)", l=BL, j=N)
-    out1_v = out_1.rearrange("(h l) (i j) c -> h (l i) (j c)", l=BL, j=N)
-    out0_v = out_0.rearrange("(h l) i c -> h (l i) c", l=BL)
+    edge_v = edge.rearrange("b (q h j) c -> (b q) h (j c)", q=Q, h=H)
+    out1_v = out_1.rearrange("b (q h j) c -> (b q) h (j c)", q=Q, h=H)
+    out0_v = out_0.rearrange("b (q h) c -> (b q) (h c)", q=Q, h=H)
+    parked_v = out_0.rearrange("b (q h) c -> b q (h c)", q=Q, h=H)
 
     with ExitStack() as ctx:
         ctx.enter_context(tc.manual_schedule())
         keep = ctx.enter_context(tc.tile_pool(name="keep", bufs=1))
-        edge_pool = ctx.enter_context(tc.tile_pool(name="edge", bufs=PREFETCH + 3))
+        edge_pool = ctx.enter_context(tc.tile_pool(name="edge", bufs=PREFETCH + 2))
         group_pool = ctx.enter_context(tc.tile_pool(name="group", bufs=2))
         code_pool = ctx.enter_context(tc.tile_pool(name="code", bufs=3))
-        msg_pool = ctx.enter_context(tc.tile_pool(name="msg", bufs=4))
+        msg_pool = ctx.enter_context(tc.tile_pool(name="msg", bufs=3))
         gate_pool = ctx.enter_context(tc.tile_pool(name="gate", bufs=2))
-        term_pool = ctx.enter_context(tc.tile_pool(name="term", bufs=1))
+        value_pool = ctx.enter_context(tc.tile_pool(name="value", bufs=3))
         junk_pool = ctx.enter_context(tc.tile_pool(name="junk", bufs=1))
         small_pool = ctx.enter_context(tc.tile_pool(name="small", bufs=3))
         tp_pool = ctx.enter_context(tc.psum_pool(name="tp", bufs=2))
         mm_pool = ctx.enter_context(tc.psum_pool(name="mm", bufs=MM_BANKS))
-        vv_pool = ctx.enter_context(tc.psum_pool(name="vv", bufs=VV_BANKS))
-        sp_pool = ctx.enter_context(tc.psum_pool(name="sp", bufs=1))
+        acc_pool = ctx.enter_context(tc.psum_pool(name="sum", bufs=1))
 
         def load_weight(words, scales, label):
             codes = keep.tile([P, G, C], I32, name=label + "_codes", align_bytes=64)
@@ -87,23 +88,26 @@ def tile_gnn_s2_pa_t_kernel(
 
         edge_tiles = {}
 
-        def load_edge(j):
-            if j not in range(N):
+        def load_edge(s):
+            if s not in range(STEPS):
                 return
-            et = edge_pool.tile([P, HALVES, C], BF16, name="et")
-            for half in range(HALVES):
-                nc.sync.dma_start(out=et[:, half, :], in_=edge_v[half, :, j * C : (j + 1) * C])
-            edge_tiles[j] = et
+            h, q = divmod(s, Q)
+            et = edge_pool.tile([P, H, C], BF16, name="et")
+            nc.sync.dma_start(out=flat(et), in_=edge_v[:, h, q * W : (q + 1) * W])
+            edge_tiles[s] = et
+
+        def flat(t):
+            return t[:].rearrange("p h c -> p (h c)")
 
         params = []
         for by_edge, by_node, label in ((bne_w, bnv_w, "w"), (bne_b, bnv_b, "b")):
-            e_bf = keep.tile([P, N], BF16, name="bne_" + label)
-            v_bf = keep.tile([P, 1], BF16, name="bnv_" + label)
+            e_bf = keep.tile([P, 2 * STEPS], BF16, name="bne_" + label)
+            v_bf = keep.tile([P, H], BF16, name="bnv_" + label)
             nc.scalar.dma_start(
-                out=e_bf[:], in_=by_edge.rearrange("(i j) -> i j", j=N).unsqueeze(0).to_broadcast([BL, N, N])
+                out=e_bf[:], in_=by_edge.rearrange("(q r) -> q r", q=Q).unsqueeze(0).to_broadcast([N, Q, 2 * STEPS])
             )
             nc.scalar.dma_start(
-                out=v_bf[:], in_=by_node.rearrange("(i o) -> i o", o=1).unsqueeze(0).to_broadcast([BL, N, 1])
+                out=v_bf[:], in_=by_node.rearrange("(q h) -> q h", q=Q).unsqueeze(0).to_broadcast([N, Q, H])
             )
             params.append((e_bf, v_bf))
 
@@ -111,30 +115,31 @@ def tile_gnn_s2_pa_t_kernel(
         nc.vector.memset(warm[:], 0.0)
         nc.scalar.activation(out=warm[:], in_=warm[:], func=ACT.Tanh)
 
-        x_sb = keep.tile([P, HALVES, C], BF16, name="x_sb")
-        nc.sync.dma_start(out=x_sb[:], in_=x.rearrange("(h l) n c -> (l n) h c", l=BL))
+        x_sb = keep.tile([P, H, C], BF16, name="x_sb")
+        nc.sync.dma_start(out=flat(x_sb), in_=x.rearrange("b (q h) c -> (b q) (h c)", q=Q, h=H))
         wa = load_weight(Wa_words, Wa_scales, "wa")
         load_edge(0)
         we = load_weight(We_words, We_scales, "we")
         wb = load_weight(Wb_words, Wb_scales, "wb")
-        for j in range(1, PREFETCH):
-            load_edge(j)
+        load_edge(1)
         wv = load_weight(Wv_words, Wv_scales, "wv")
+        for s in range(2, PREFETCH):
+            load_edge(s)
         wu = load_weight(Wu_words, Wu_scales, "wu")
 
         ident = keep.tile([P, P], F32, name="ident")
         make_identity(nc, ident[:])
-        same_i = keep.tile([P, N], F32, name="same_i")
+        same_i = keep.tile([P, Q], F32, name="same_i")
         nc.vector.tensor_reduce(
-            out=same_i[:], in_=ident[:].rearrange("p (l i) -> p i l", l=BL), axis=AX.X, op=ALU.add
+            out=same_i[:], in_=ident[:].rearrange("p (b q) -> p q b", q=Q), axis=AX.X, op=ALU.add
         )
-        group_mean = keep.tile([P, BL, N], F32, name="group_mean")
+        group_mean = keep.tile([P, N, Q], F32, name="group_mean")
         nc.vector.tensor_scalar_mul(
-            out=group_mean[:], in0=same_i[:].unsqueeze(1).to_broadcast([P, BL, N]), scalar1=-1.0 / COUNT
+            out=group_mean[:], in0=same_i[:].unsqueeze(1).to_broadcast([P, N, Q]), scalar1=1.0 / COUNT
         )
-        minus_half = keep.tile([P, 1], F32, name="minus_half")
+        minus_half = keep.tile([P, H], F32, name="minus_half")
         nc.vector.memset(minus_half[:], -0.5)
-        stats = keep.tile([P, N + 1, 32], F32, name="stats")
+        stats = keep.tile([P, STEPS + 1, H * 4], F32, name="stats")
         nc.vector.memset(stats[:], 0.0)
 
         def transpose_words(bank, rows):
@@ -145,52 +150,51 @@ def tile_gnn_s2_pa_t_kernel(
                         out=bank[:, g, u, :], in_=words[:, 256 * g + u : 256 * (g + 1) : 2], identity=ident[:]
                     )
 
-        xg = keep.tile([P, G * HALVES * P * 4], BF16, name="xg", align_bytes=64)
-        xg_words = xg[:].bitcast(F32).rearrange("p (g h r u) -> p g h r u", g=G, h=HALVES, u=2)
-        xs4 = keep.tile([P, G * HALVES * P * 4], U8, name="xs4", align_bytes=64)
+        xg = keep.tile([P, G * H * P * 4], BF16, name="xg", align_bytes=64)
+        xg_words = xg[:].bitcast(F32).rearrange("p (g h r u) -> p g h r u", g=G, h=H, u=2)
+        xs4 = keep.tile([P, G * H * P * 4], U8, name="xs4", align_bytes=64)
         nc.vector.memset(xs4[:].bitcast(I32), 0)
         x_banks = []
-        for half in range(HALVES):
+        for h in range(H):
             bank = tp_pool.tile([P, G, 2, P], F32, name="bank")
-            transpose_words(bank, x_sb[:, half, :])
-            nc.vector.tensor_copy(out=xg_words[:, :, half], in_=bank[:].rearrange("p g u r -> p g r u"))
+            transpose_words(bank, x_sb[:, h, :])
+            nc.vector.tensor_copy(out=xg_words[:, :, h], in_=bank[:].rearrange("p g u r -> p g r u"))
             x_banks.append(bank)
-        xq = keep.tile([P, G * HALVES * P], I32, name="xq", align_bytes=64)
-        xs = keep.tile([P, G * HALVES * P], U8, name="xs", align_bytes=64)
+        xq = keep.tile([P, G * H * P], I32, name="xq", align_bytes=64)
+        xs = keep.tile([P, G * H * P], U8, name="xs", align_bytes=64)
         nc.vector.quantize_mx(out=xq[:].bitcast(FP8X4), scales=xs[:], in_=xg[:])
-        for half in range(HALVES):
+        for h in range(H):
             for g in range(G):
                 eg = group_pool.tile([P, P * 4 * 4], BF16, name="eg", align_bytes=64)
                 nc.scalar.copy(
                     out=eg[:].bitcast(F32).rearrange("p (r f u) -> p r f u", f=4, u=2),
-                    in_=x_banks[half][:, g].rearrange("p u r -> p r u").unsqueeze(2).to_broadcast([P, P, 4, 2]),
+                    in_=x_banks[h][:, g].rearrange("p u r -> p r u").unsqueeze(2).to_broadcast([P, P, 4, 2]),
                 )
                 eq = code_pool.tile([P, P * 4], I32, name="eq", align_bytes=64)
-                block = slice((g * HALVES + half) * P * 4, (g * HALVES + half + 1) * P * 4)
+                block = slice((g * H + h) * P * 4, (g * H + h + 1) * P * 4)
                 nc.vector.quantize_mx(out=eq[:].bitcast(FP8X4), scales=xs4[:, block], in_=eg[:])
 
-        gain = keep.tile([P, N + 1], F32, name="gain")
-        shift = keep.tile([P, N + 1], F32, name="shift")
+        gain = keep.tile([P, 2 * STEPS + H], F32, name="gain")
+        shift = keep.tile([P, 2 * STEPS + H], F32, name="shift")
         for dst, (e_bf, v_bf) in zip((gain, shift), params):
-            nc.vector.tensor_copy(out=dst[:, 0:N], in_=e_bf[:])
-            nc.vector.tensor_copy(out=dst[:, N : N + 1], in_=v_bf[:])
+            nc.vector.tensor_copy(out=dst[:, 0 : 2 * STEPS], in_=e_bf[:])
+            nc.vector.tensor_copy(out=dst[:, 2 * STEPS :], in_=v_bf[:])
 
-        xr = keep.tile([P, N, G * HALVES * P], I32, name="xr", align_bytes=64)
-        xrs = keep.tile([P, N, G * HALVES * P], U8, name="xrs", align_bytes=64)
-        xq_v = xq[:].rearrange("p (a l n) -> p n a l", a=G * HALVES, l=BL)
-        xs4_v = xs4[:].bitcast(I32).rearrange("p (a l n) -> p n a l", a=G * HALVES, l=BL)
+        xr = keep.tile([P, Q, G * H * P], I32, name="xr", align_bytes=64)
+        xrs = keep.tile([P, Q, G * H * P], U8, name="xrs", align_bytes=64)
+        xq_v = xq[:].rearrange("p (a q) -> p q a", q=Q)
+        xs4_v = xs4[:].bitcast(I32).rearrange("p (a q) -> p q a", q=Q)
 
-        def repeat_nodes(block):
-            if block not in range(N // REP):
+        def repeat_nodes(q):
+            if q not in range(Q):
                 return
-            js = slice(block * REP, (block + 1) * REP)
             nc.vector.tensor_copy(
-                out=xr[:, js, :].rearrange("p j (a l i) -> p j a l i", a=G * HALVES, l=BL),
-                in_=xq_v[:, js].unsqueeze(4).to_broadcast([P, REP, G * HALVES, BL, N]),
+                out=xr[:, q, :].rearrange("p (a i) -> p a i", i=Q),
+                in_=xq_v[:, q].unsqueeze(2).to_broadcast([P, G * H * N, Q]),
             )
             nc.vector.tensor_copy(
-                out=xrs[:, js, :].bitcast(I32).rearrange("p j (a l w) -> p j a l w", a=G * HALVES, l=BL),
-                in_=xs4_v[:, js].unsqueeze(4).to_broadcast([P, REP, G * HALVES, BL, 4]),
+                out=xrs[:, q, :].bitcast(I32).rearrange("p (a w) -> p a w", w=2),
+                in_=xs4_v[:, q].unsqueeze(2).to_broadcast([P, G * H * N, 2]),
             )
 
         def mx_passes(acc, stationary, weights, cols, first, last):
@@ -207,249 +211,315 @@ def tile_gnn_s2_pa_t_kernel(
                     stop=last and g == G - 1,
                 )
 
-        def block_of(codes, plane, half):
+        def block_of(codes, plane, h):
             def cut(t):
-                return lambda g: t[:, (g * HALVES + half) * P : (g * HALVES + half + 1) * P]
+                return lambda g: t[:, (g * H + h) * P : (g * H + h + 1) * P]
 
             return cut(codes), cut(plane)
 
         def columns(k):
             return slice((k % 2) * BANK, (k % 2 + 1) * BANK)
 
-        def flat(t):
-            return t[:].rearrange("p h c -> p (h c)")
-
-        def pieces(j):
-            count = QUARTERS if j == N - 1 else 1
-            width = HALVES * C // count
-            return [slice(i * width, (i + 1) * width) for i in range(count)]
-
-        ax = keep.tile([P, C], F32, name="ax")
-        for k in range(QUARTERS // 2):
+        def product(dst, weights, k):
             acc = mm_pool.tile([P, BANK], F32, name="acc")
-            mx_passes(acc, block_of(xq, xs, 0), wa, columns(k), True, True)
-            nc.scalar.copy(out=ax[:, columns(k)], in_=acc[:])
+            mx_passes(acc, block_of(xq, xs, k // 2), weights, columns(k), True, True)
+            nc.scalar.copy(out=dst[:, k // 2, columns(k)], in_=acc[:])
+
+        ax = keep.tile([P, H, C], F32, name="ax")
+        for k in range(QUARTERS):
+            product(ax, wa, k)
+        park = value_pool.tile([P, H, C], F32, name="vt")
+        ux = keep.tile([P, H, C], F32, name="ux")
 
         flipped = {}
         groups = {}
         codes = {}
         banks = {}
-        values = {}
         msgs = {}
         gates = {}
-        terms = {}
+        values = {}
         coeffs = {}
-        den = keep.tile([P, HALVES, C], F32, name="den")
-        num = keep.tile([P, HALVES, C], F32, name="num")
+        totals = {}
+        sums_t = {}
 
-        def transpose_edge(j):
-            if j not in range(N):
+        def transpose_edge(s):
+            if s not in range(STEPS):
                 return
-            for half in range(HALVES):
+            for h in range(H):
                 bank = tp_pool.tile([P, G, 2, P], F32, name="bank")
-                transpose_words(bank, edge_tiles[j][:, half, :])
-                flipped[j, half] = bank
+                transpose_words(bank, edge_tiles[s][:, h, :])
+                flipped[s, h] = bank
 
-        def group_edge(j):
-            if j not in range(N):
+        def group_edge(s):
+            if s not in range(STEPS):
                 return
-            eg = group_pool.tile([P, G * HALVES * P * 4], BF16, name="eg", align_bytes=64)
-            eg_words = eg[:].bitcast(F32).rearrange("p (g h r u) -> p g h r u", g=G, h=HALVES, u=2)
-            for half in range(HALVES):
-                nc.scalar.copy(out=eg_words[:, :, half], in_=flipped[j, half][:].rearrange("p g u r -> p g r u"))
-            groups[j] = eg
+            eg = group_pool.tile([P, G * H * P * 4], BF16, name="eg", align_bytes=64)
+            eg_words = eg[:].bitcast(F32).rearrange("p (g h r u) -> p g h r u", g=G, h=H, u=2)
+            for h in range(H):
+                nc.scalar.copy(out=eg_words[:, :, h], in_=flipped[s, h][:].rearrange("p g u r -> p g r u"))
+            groups[s] = eg
 
-        def quantise_edge(j):
-            if j not in range(N):
+        def quantise_edge(s):
+            if s not in range(STEPS):
                 return
-            eq = code_pool.tile([P, G * HALVES * P], I32, name="eq", align_bytes=64)
-            es = code_pool.tile([P, G * HALVES * P], U8, name="es", align_bytes=64)
-            nc.vector.quantize_mx(out=eq[:].bitcast(FP8X4), scales=es[:], in_=groups[j][:])
-            codes[j] = (eq, es)
+            eq = code_pool.tile([P, G * H * P], I32, name="eq", align_bytes=64)
+            es = code_pool.tile([P, G * H * P], U8, name="es", align_bytes=64)
+            nc.vector.quantize_mx(out=eq[:].bitcast(FP8X4), scales=es[:], in_=groups[s][:])
+            codes[s] = (eq, es)
 
-        def fill_message_bank(q):
-            if q not in range(N * QUARTERS):
+        def fill_message_bank(n):
+            if n not in range(STEPS * QUARTERS):
                 return
-            j, k = divmod(q, QUARTERS)
+            s, k = divmod(n, QUARTERS)
             acc = mm_pool.tile([P, BANK], F32, name="acc")
-            mx_passes(acc, block_of(codes[j][0], codes[j][1], k // 2), we, columns(k), True, False)
-            if k // 2 == 1:
-                mx_passes(acc, block_of(xq, xs, 1), wa, columns(k), False, False)
-            mx_passes(acc, block_of(xr[:, j, :], xrs[:, j, :], k // 2), wb, columns(k), False, True)
-            banks[q] = acc
+            mx_passes(acc, block_of(codes[s][0], codes[s][1], k // 2), we, columns(k), True, False)
+            mx_passes(acc, block_of(xr[:, s % Q, :], xrs[:, s % Q, :], k // 2), wb, columns(k), False, True)
+            banks[n] = acc
 
-        def evacuate(j, k):
-            if j not in range(N):
+        def evacuate(s, k):
+            if s not in range(STEPS):
                 return
             if k == 0:
-                msgs[j] = msg_pool.tile([P, HALVES, C], F32, name="msg")
-            if k // 2 == 0:
-                nc.vector.scalar_tensor_tensor(
-                    out=msgs[j][:, 0, columns(k)],
-                    in0=banks[QUARTERS * j + k][:],
-                    scalar=1.0,
-                    in1=ax[:, columns(k)],
-                    op0=ALU.mult,
-                    op1=ALU.add,
-                    accum_out=stats[:, j, k : k + 1],
-                )
-            else:
-                nc.scalar.activation(
-                    out=msgs[j][:, 1, columns(k)],
-                    in_=banks[QUARTERS * j + k][:],
-                    func=ACT.Identity,
-                    accum_out=stats[:, j, 8 + k % 2 : 9 + k % 2],
-                )
+                msgs[s] = msg_pool.tile([P, H, C], F32, name="msg")
+            nc.vector.scalar_tensor_tensor(
+                out=msgs[s][:, k // 2, columns(k)],
+                in0=banks[QUARTERS * s + k][:],
+                scalar=1.0,
+                in1=ax[:, s // Q, columns(k)],
+                op0=ALU.mult,
+                op1=ALU.add,
+                accum_out=stats[:, s, 4 * (k // 2) + k % 2 : 4 * (k // 2) + k % 2 + 1],
+            )
 
-        def square_sum(values_tile, row, ranges):
-            junk = junk_pool.tile([P, HALVES, C], BF16, name="junk")
-            for index, cols in enumerate(ranges):
+        def early_products(t, k):
+            if t == 0:
+                product(park, wv, k)
+                if k == QUARTERS - 1:
+                    nc.sync.dma_start(out=out0_v, in_=flat(park))
+            if t == 2:
+                product(ux, wu, k)
+
+        def square_sum(rows, row, tile_index, parts):
+            width = C // parts
+            junk = junk_pool.tile([P, C], BF16, name="junk")
+            for part in range(parts):
+                col = 4 * tile_index + 2 + part
                 nc.scalar.activation(
-                    out=flat(junk)[:, cols],
-                    in_=flat(values_tile)[:, cols],
+                    out=junk[:, part * width : (part + 1) * width],
+                    in_=rows[:, part * width : (part + 1) * width],
                     func=ACT.Square,
-                    accum_out=stats[:, row, 16 + index : 17 + index],
+                    accum_out=stats[:, row, col : col + 1],
                 )
 
-        def stat_sums(row):
-            sums = sp_pool.tile([P, 32], F32, name="sums")
+        def group_sums(row):
+            sums = tp_pool.tile([P, H * 4], F32, name="bank")
             nc.tensor.matmul(
-                out=sums[:], lhsT=group_mean[:].rearrange("p l i -> p (l i)"), rhs=stats[:, row, :], start=True, stop=True
+                out=sums[:], lhsT=group_mean[:].rearrange("p b q -> p (b q)"), rhs=stats[:, row, :], start=True, stop=True
             )
             return sums
 
-        def coefficients(sums, row):
-            neg = small_pool.tile([P, 2], F32, name="neg")
-            nc.vector.tensor_reduce(out=neg[:], in_=sums[:].rearrange("p (a b) -> p a b", a=2), axis=AX.X, op=ALU.add)
-            nvar = small_pool.tile([P, 1], F32, name="nvar")
-            nc.gpsimd.tensor_scalar(
-                out=nvar[:], in0=neg[:, 0:1], scalar1=neg[:, 0:1], scalar2=neg[:, 1:2], op0=ALU.mult, op1=ALU.add
+        def moments_of(sums):
+            moments = small_pool.tile([P, 2, H], F32, name="moments")
+            nc.vector.tensor_reduce(
+                out=moments[:], in_=sums[:].rearrange("p (h k t) -> p k h t", k=2, t=2), axis=AX.X, op=ALU.add
             )
-            vpe = small_pool.tile([P, 1], F32, name="vpe")
-            nc.gpsimd.tensor_scalar(out=vpe[:], in0=nvar[:], scalar1=-1.0, scalar2=EPS, op0=ALU.mult, op1=ALU.add)
-            safe = small_pool.tile([P, 1], F32, name="safe")
-            nc.gpsimd.tensor_scalar_max(out=safe[:], in0=vpe[:], scalar1=EPS)
-            rstd = small_pool.tile([P, 1], F32, name="rstd")
-            nc.gpsimd.tensor_tensor(out=rstd[:], in0=safe[:], in1=minus_half[:], op=ALU.pow)
-            scale = small_pool.tile([P, 1], F32, name="scale")
-            nc.gpsimd.tensor_tensor(out=scale[:], in0=rstd[:], in1=gain[:, row : row + 1], op=ALU.mult)
-            offset = small_pool.tile([P, 1], F32, name="offset")
+            return moments
+
+        def coefficients(moments, col, gains, shifts):
+            mean, square = moments[:, 0, col], moments[:, 1, col]
+            width = col.stop - col.start
+            sq_mean = small_pool.tile([P, H], F32, name="sq_mean")
+            nc.gpsimd.tensor_tensor(out=sq_mean[:, 0:width], in0=mean, in1=mean, op=ALU.mult)
+            var = small_pool.tile([P, H], F32, name="var")
+            nc.gpsimd.tensor_tensor(out=var[:, 0:width], in0=square, in1=sq_mean[:, 0:width], op=ALU.subtract)
+            safe = small_pool.tile([P, H], F32, name="safe")
             nc.gpsimd.tensor_scalar(
-                out=offset[:],
-                in0=neg[:, 0:1],
-                scalar1=scale[:],
-                scalar2=shift[:, row : row + 1],
-                op0=ALU.mult,
-                op1=ALU.add,
+                out=safe[:, 0:width], in0=var[:, 0:width], scalar1=0.0, scalar2=EPS, op0=ALU.max, op1=ALU.add
             )
+            rstd = small_pool.tile([P, H], F32, name="rstd")
+            nc.gpsimd.tensor_tensor(out=rstd[:, 0:width], in0=safe[:, 0:width], in1=minus_half[:, 0:width], op=ALU.pow)
+            scale = small_pool.tile([P, H], F32, name="scale")
+            nc.gpsimd.tensor_tensor(out=scale[:, 0:width], in0=rstd[:, 0:width], in1=gains, op=ALU.mult)
+            drift = small_pool.tile([P, H], F32, name="drift")
+            nc.gpsimd.tensor_tensor(out=drift[:, 0:width], in0=mean, in1=scale[:, 0:width], op=ALU.mult)
+            offset = small_pool.tile([P, H], F32, name="offset")
+            nc.gpsimd.tensor_tensor(out=offset[:, 0:width], in0=shifts, in1=drift[:, 0:width], op=ALU.subtract)
             return scale, offset
 
-        def normalise(j):
-            if j not in range(N):
+        sums_of = {}
+
+        def edge_sums(s):
+            if s in range(STEPS):
+                sums_of[s] = group_sums(s)
+
+        def edge_coefficients(s):
+            if s not in range(STEPS):
                 return
-            scale, offset = coeffs[j]
-            for cols in pieces(j):
-                nc.scalar.activation(
-                    out=flat(msgs[j])[:, cols], in_=flat(msgs[j])[:, cols], func=ACT.Relu, scale=scale[:], bias=offset[:]
+            cols = slice(H * s, H * s + H)
+            coeffs[s] = coefficients(moments_of(sums_of[s]), slice(0, H), gain[:, cols], shift[:, cols])
+
+        def normalise(s):
+            if s not in range(STEPS):
+                return
+            scale, offset = coeffs[s]
+            for h in range(H):
+                nc.vector.tensor_scalar(
+                    out=msgs[s][:, h, :],
+                    in0=msgs[s][:, h, :],
+                    scalar1=scale[:, h : h + 1],
+                    scalar2=offset[:, h : h + 1],
+                    op0=ALU.mult,
+                    op1=ALU.add,
                 )
 
-        def finish_edge(j):
-            if j not in range(N):
+        def pieces(s):
+            count = QUARTERS if s == STEPS - 1 else H
+            return [slice(i * W // count, (i + 1) * W // count) for i in range(count)]
+
+        def finish_edge(s):
+            if s not in range(STEPS):
                 return
-            for cols in pieces(j):
+            for cols in pieces(s):
+                nc.vector.scalar_tensor_tensor(
+                    out=flat(msgs[s])[:, cols],
+                    in0=flat(msgs[s])[:, cols],
+                    scalar=0.0,
+                    in1=flat(edge_tiles[s])[:, cols],
+                    op0=ALU.max,
+                    op1=ALU.add,
+                )
+            q = s % Q
+            nc.sync.dma_start(out=out1_v[:, s // Q, q * W : (q + 1) * W], in_=flat(msgs[s]))
+
+        def weights_of(s):
+            if s not in range(STEPS):
+                return
+            gates[s] = gate_pool.tile([P, H, C], F32, name="gate")
+            gate = flat(gates[s])
+            for cols in pieces(s):
+                nc.scalar.activation(out=gate[:, cols], in_=flat(msgs[s])[:, cols], func=ACT.Tanh, scale=0.5)
+                nc.scalar.activation(out=gate[:, cols], in_=gate[:, cols], func=ACT.Exp, scale=0.5)
+
+        def load_values(s):
+            if s not in range(STEPS):
+                return
+            vt = value_pool.tile([P, H, C], F32, name="vt")
+            nc.sync.dma_start(out=flat(vt), in_=parked_v[:, s % Q, :].unsqueeze(1).to_broadcast([N, Q, W]))
+            values[s] = vt
+
+        def weigh_values(s, h):
+            if s not in range(STEPS):
+                return
+            for cols in pieces(s)[h * len(pieces(s)) // H : (h + 1) * len(pieces(s)) // H]:
                 nc.vector.tensor_tensor(
-                    out=flat(msgs[j])[:, cols], in0=flat(msgs[j])[:, cols], in1=flat(edge_tiles[j])[:, cols], op=ALU.add
-                )
-            for half in range(HALVES):
-                nc.sync.dma_start(out=out1_v[half, :, j * C : (j + 1) * C], in_=msgs[j][:, half, :])
-            gate = gate_pool.tile([P, HALVES, C], F32, name="gate")
-            for cols in pieces(j):
-                nc.scalar.activation(out=flat(gate)[:, cols], in_=flat(msgs[j])[:, cols], func=ACT.Tanh, scale=0.5)
-            gates[j] = den if j == 0 else gate
-            for cols in pieces(j):
-                nc.scalar.activation(out=flat(gates[j])[:, cols], in_=flat(gate)[:, cols], func=ACT.Exp, scale=0.5)
-
-        def fill_value_bank(q):
-            if q not in range(N * QUARTERS):
-                return
-            j, k = divmod(q, QUARTERS)
-            acc = vv_pool.tile([P, BANK], F32, name="vrep")
-            mx_passes(acc, block_of(xr[:, j, :], xrs[:, j, :], k // 2), wv, columns(k), True, True)
-            values[q] = acc
-
-        def add_to_denominator(j):
-            if j not in range(1, N):
-                return
-            for cols in pieces(j):
-                nc.vector.tensor_tensor(
-                    out=flat(den)[:, cols], in0=flat(den)[:, cols], in1=flat(gates[j])[:, cols], op=ALU.add
+                    out=flat(values[s])[:, cols], in0=flat(values[s])[:, cols], in1=flat(gates[s])[:, cols], op=ALU.mult
                 )
 
-        def weigh_values(j, k):
-            if j not in range(N):
+        def sum_over_j(label, s, tile):
+            if s not in range(STEPS):
                 return
-            if k == 0:
-                terms[j] = num if j == 0 else term_pool.tile([P, HALVES, C], F32, name="term")
-            nc.vector.tensor_tensor(
-                out=terms[j][:, k // 2, columns(k)],
-                in0=values[QUARTERS * j + k][:],
-                in1=gates[j][:, k // 2, columns(k)],
-                op=ALU.mult,
-            )
+            half, q = divmod(s, Q)
+            per_bank = BANK // P
+            if q == 0:
+                sums_t[label, half] = [
+                    acc_pool.tile([P, per_bank, P], F32, name=label + str(b)) for b in range(C // BANK)
+                ]
+            for h in range(H):
+                for chunk in range(CHUNKS):
+                    b, place = divmod(chunk, per_bank)
+                    nc.tensor.matmul(
+                        out=sums_t[label, half][b][:, place, :],
+                        lhsT=tile[:, h, chunk * P : (chunk + 1) * P],
+                        rhs=ident[:],
+                        is_transpose=True,
+                        start=q == 0 and h == 0 and place == 0,
+                        stop=q == Q - 1 and h == H - 1 and place == per_bank - 1,
+                    )
 
-        def add_to_numerator(j, half):
-            if j not in range(1, N):
+        def finish_sums(label, s):
+            if s not in (Q - 1, STEPS - 1):
                 return
-            nc.vector.tensor_tensor(out=num[:, half, :], in0=num[:, half, :], in1=terms[j][:, half, :], op=ALU.add)
+            half = s // Q
+            pieces_t = [bank[:].rearrange("p k r -> p (k r)") for bank in sums_t[label, half]]
+            if half == 0:
+                t = keep.tile([P, C], F32, name=label + "_t")
+                for b in range(C // BANK):
+                    cols = slice(b * BANK, (b + 1) * BANK)
+                    nc.scalar.copy(out=t[:, cols], in_=pieces_t[b])
+                    pieces_t[b] = t[:, cols]
+            totals[label, half] = pieces_t
 
-        for t in range(-3, N + 3):
+        for t in range(-3, STEPS + 2):
             if t >= 0:
                 load_edge(t + PREFETCH)
-            repeat_nodes(t + 3)
-            normalise(t - 2)
-            for k in range(QUARTERS):
+            load_values(t - 1)
+            repeat_nodes(t + 2)
+            for k in (0, 1):
                 evacuate(t, k)
+                early_products(t, k)
                 fill_message_bank(QUARTERS * t + k + MM_BANKS)
-            if t in range(N):
-                square_sum(msgs[t], t, pieces(t))
+            weigh_values(t - 2, 0)
+            sum_over_j("den", t - 2, gates.get(t - 2))
+            finish_sums("den", t - 2)
+            if t in range(STEPS):
+                square_sum(msgs[t][:, 0, :], t, 0, 1)
+            for k in (2, 3):
+                evacuate(t, k)
+                early_products(t, k)
+                fill_message_bank(QUARTERS * t + k + MM_BANKS)
+            weigh_values(t - 2, 1)
             group_edge(t + 2)
-            add_to_denominator(t - 3)
-            finish_edge(t - 2)
-            if t in range(N):
-                sums = stat_sums(t)
-            for k in range(QUARTERS):
-                weigh_values(t - 3, k)
-                fill_value_bank(QUARTERS * (t - 3) + k + VV_BANKS)
-                if k == 1:
-                    if t in range(N):
-                        coeffs[t] = coefficients(sums, t)
-                    add_to_numerator(t - 3, 0)
-            quantise_edge(t + 2)
-            add_to_numerator(t - 3, 1)
+            if t in range(STEPS):
+                square_sum(msgs[t][:, 1, :], t, 1, 1)
+            normalise(t - 1)
+            finish_edge(t - 1)
+            weights_of(t - 1)
+            sum_over_j("num", t - 2, values.get(t - 2))
+            finish_sums("num", t - 2)
+            edge_sums(t)
             transpose_edge(t + 3)
+            edge_coefficients(t)
+            quantise_edge(t + 2)
 
-        y = msg_pool.tile([P, HALVES, C], F32, name="msg")
-        for k in range(QUARTERS):
-            part = (slice(None), k // 2, columns(k))
-            nc.scalar.activation(out=den[part], in_=den[part], func=ACT.Abs_reciprocal_sqrt, scale=float(N))
-            nc.scalar.activation(out=den[part], in_=den[part], func=ACT.Square)
-            nc.vector.tensor_tensor(out=num[part], in0=num[part], in1=den[part], op=ALU.mult)
-            acc = mm_pool.tile([P, BANK], F32, name="acc")
-            mx_passes(acc, block_of(xq, xs, k // 2), wu, columns(k), True, True)
+        y = msg_pool.tile([P, H, C], F32, name="msg")
+        act = gate_pool.tile([P, H, C], F32, name="gate")
+        quo = keep.tile([P, H, C], F32, name="quo")
+        quarters = [(half, k, slice(k * BANK, (k + 1) * BANK)) for half in range(H) for k in range(C // BANK)]
+        for half, k, cols in quarters:
+            nc.scalar.activation(
+                out=quo[:, half, cols], in_=totals["den", half][k], func=ACT.Abs_reciprocal_sqrt, scale=float(N)
+            )
+            nc.scalar.activation(out=quo[:, half, cols], in_=quo[:, half, cols], func=ACT.Square)
+        for half, k, cols in quarters:
+            nc.vector.tensor_tensor(
+                out=quo[:, half, cols], in0=totals["num", half][k], in1=quo[:, half, cols], op=ALU.mult
+            )
+            back = mm_pool.tile([P, BANK], F32, name="acc")
+            for place in range(BANK // P):
+                nc.tensor.transpose(
+                    out=back[:, place * P : (place + 1) * P],
+                    in_=quo[:, half, k * BANK + place * P : k * BANK + (place + 1) * P],
+                    identity=ident[:],
+                )
             nc.vector.scalar_tensor_tensor(
-                out=y[part],
-                in0=acc[:],
+                out=y[:, half, cols],
+                in0=back[:],
                 scalar=1.0,
-                in1=num[part],
+                in1=ux[:, half, cols],
                 op0=ALU.mult,
                 op1=ALU.add,
-                accum_out=stats[:, N, k : k + 1],
+                accum_out=stats[:, STEPS, 4 * half + k : 4 * half + k + 1],
             )
-        square_sum(y, N, pieces(N - 1))
-        scale, offset = coefficients(stat_sums(N), N)
-        act = gate_pool.tile([P, HALVES, C], F32, name="gate")
-        for k in range(QUARTERS):
-            part = (slice(None), k // 2, columns(k))
-            nc.scalar.activation(out=act[part], in_=y[part], func=ACT.Relu, scale=scale[:], bias=offset[:])
-            nc.vector.tensor_tensor(out=y[part], in0=y[part], in1=act[part], op=ALU.add)
-            nc.sync.dma_start(out=out0_v[k // 2, :, columns(k)], in_=y[part])
+            if k == C // BANK - 1:
+                square_sum(y[:, half, :], STEPS, half, 2)
+        scale, offset = coefficients(moments_of(group_sums(STEPS)), slice(0, H), gain[:, 2 * STEPS :], shift[:, 2 * STEPS :])
+        for half, k, cols in quarters:
+            nc.scalar.activation(
+                out=act[:, half, cols],
+                in_=y[:, half, cols],
+                func=ACT.Relu,
+                scale=scale[:, half : half + 1],
+                bias=offset[:, half : half + 1],
+            )
+            nc.vector.tensor_tensor(out=y[:, half, cols], in0=y[:, half, cols], in1=act[:, half, cols], op=ALU.add)
+            nc.sync.dma_start(out=out0_v[:, half * C + k * BANK : half * C + (k + 1) * BANK], in_=y[:, half, cols])

@@ -74,8 +74,8 @@ def tile_gnn_s2_pa_t_kernel(
         mm_pool = ctx.enter_context(tc.psum_pool(name="mm", bufs=MM_BANKS))
         acc_pool = ctx.enter_context(tc.psum_pool(name="sum", bufs=1))
 
-        def load_weight(words, scales, label):
-            codes = keep.tile([P, G, C], I32, name=label + "_codes", align_bytes=64)
+        def start_weight(scales, label):
+            halves = [keep.tile([P, G, BANK], I32, name=label + "_codes" + str(c), align_bytes=64) for c in range(2)]
             plane = keep.tile([P, G, C], U8, name=label + "_plane", align_bytes=64)
             nc.vector.memset(plane[:].rearrange("p g n -> p (g n)").bitcast(I32), 0)
             for quad in range(4):
@@ -83,8 +83,13 @@ def tile_gnn_s2_pa_t_kernel(
                     out=plane[32 * quad : 32 * quad + 4, :, :].bitcast(I32),
                     in_=scales[:, 4 * quad : 4 * quad + 4, :].rearrange("g r n -> r g n").bitcast(I32),
                 )
-            nc.sync.dma_start(out=codes[:], in_=words.rearrange("g p n t -> p g (n t)").bitcast(I32))
-            return codes, plane
+            return halves, plane
+
+        def load_codes(weight, words, c):
+            nc.sync.dma_start(
+                out=weight[0][c][:],
+                in_=words[:, :, c * BANK : (c + 1) * BANK, :].rearrange("g p n t -> p g (n t)").bitcast(I32),
+            )
 
         edge_tiles = {}
 
@@ -117,15 +122,24 @@ def tile_gnn_s2_pa_t_kernel(
 
         x_sb = keep.tile([P, H, C], BF16, name="x_sb")
         nc.sync.dma_start(out=flat(x_sb), in_=x.rearrange("b (q h) c -> (b q) (h c)", q=Q, h=H))
-        wa = load_weight(Wa_words, Wa_scales, "wa")
         load_edge(0)
-        we = load_weight(We_words, We_scales, "we")
-        wb = load_weight(Wb_words, Wb_scales, "wb")
+        wa = start_weight(Wa_scales, "wa")
+        we = start_weight(We_scales, "we")
+        wb = start_weight(Wb_scales, "wb")
+        for c in range(2):
+            load_codes(wa, Wa_words, c)
+            load_codes(we, We_words, c)
+            load_codes(wb, Wb_words, c)
         load_edge(1)
-        wv = load_weight(Wv_words, Wv_scales, "wv")
-        for s in range(2, PREFETCH):
+        load_edge(2)
+        wv = start_weight(Wv_scales, "wv")
+        for c in range(2):
+            load_codes(wv, Wv_words, c)
+        for s in range(3, PREFETCH):
             load_edge(s)
-        wu = load_weight(Wu_words, Wu_scales, "wu")
+        wu = start_weight(Wu_scales, "wu")
+        for c in range(2):
+            load_codes(wu, Wu_words, c)
 
         ident = keep.tile([P, P], F32, name="ident")
         make_identity(nc, ident[:])
@@ -153,26 +167,17 @@ def tile_gnn_s2_pa_t_kernel(
         xg = keep.tile([P, G * H * P * 4], BF16, name="xg", align_bytes=64)
         xg_words = xg[:].bitcast(F32).rearrange("p (g h r u) -> p g h r u", g=G, h=H, u=2)
         xs4 = keep.tile([P, G * H * P * 4], U8, name="xs4", align_bytes=64)
-        nc.vector.memset(xs4[:].bitcast(I32), 0)
-        x_banks = []
         for h in range(H):
             bank = tp_pool.tile([P, G, 2, P], F32, name="bank")
             transpose_words(bank, x_sb[:, h, :])
             nc.vector.tensor_copy(out=xg_words[:, :, h], in_=bank[:].rearrange("p g u r -> p g r u"))
-            x_banks.append(bank)
         xq = keep.tile([P, G * H * P], I32, name="xq", align_bytes=64)
         xs = keep.tile([P, G * H * P], U8, name="xs", align_bytes=64)
+        nc.vector.memset(xs[:].bitcast(I32), 0)
         nc.vector.quantize_mx(out=xq[:].bitcast(FP8X4), scales=xs[:], in_=xg[:])
-        for h in range(H):
-            for g in range(G):
-                eg = group_pool.tile([P, P * 4 * 4], BF16, name="eg", align_bytes=64)
-                nc.scalar.copy(
-                    out=eg[:].bitcast(F32).rearrange("p (r f u) -> p r f u", f=4, u=2),
-                    in_=x_banks[h][:, g].rearrange("p u r -> p r u").unsqueeze(2).to_broadcast([P, P, 4, 2]),
-                )
-                eq = code_pool.tile([P, P * 4], I32, name="eq", align_bytes=64)
-                block = slice((g * H + h) * P * 4, (g * H + h + 1) * P * 4)
-                nc.vector.quantize_mx(out=eq[:].bitcast(FP8X4), scales=xs4[:, block], in_=eg[:])
+        xs4_bytes = xs4[:].rearrange("p (a f) -> p a f", f=4)
+        for copy in range(4):
+            nc.vector.tensor_copy(out=xs4_bytes[:, :, copy], in_=xs[:])
 
         gain = keep.tile([P, 2 * STEPS + H], F32, name="gain")
         shift = keep.tile([P, 2 * STEPS + H], F32, name="shift")
@@ -197,7 +202,7 @@ def tile_gnn_s2_pa_t_kernel(
                 in_=xs4_v[:, q].unsqueeze(2).to_broadcast([P, G * H * N, 2]),
             )
 
-        def mx_passes(acc, stationary, weights, cols, first, last):
+        def mx_passes(acc, stationary, weights, c, first, last):
             s_codes, s_plane = stationary
             w_codes, w_plane = weights
             for g in range(G):
@@ -205,8 +210,8 @@ def tile_gnn_s2_pa_t_kernel(
                     out=acc[:],
                     lhsT=s_codes(g).bitcast(FP8X4),
                     lhsT_scale=s_plane(g),
-                    rhs=w_codes[:, g, cols].bitcast(FP8X4),
-                    rhs_scale=w_plane[:, g, cols],
+                    rhs=w_codes[c][:, g, :].bitcast(FP8X4),
+                    rhs_scale=w_plane[:, g, columns(c)],
                     start=first and g == 0,
                     stop=last and g == G - 1,
                 )
@@ -220,14 +225,16 @@ def tile_gnn_s2_pa_t_kernel(
         def columns(k):
             return slice((k % 2) * BANK, (k % 2 + 1) * BANK)
 
-        def product(dst, weights, k):
-            acc = mm_pool.tile([P, BANK], F32, name="acc")
-            mx_passes(acc, block_of(xq, xs, k // 2), weights, columns(k), True, True)
-            nc.scalar.copy(out=dst[:, k // 2, columns(k)], in_=acc[:])
+        def product(dst, weights, h, c, acc, copy):
+            mx_passes(acc, block_of(xq, xs, h), weights, c, True, True)
+            copy(out=dst[:, h, columns(c)], in_=acc[:])
+
+        def node_product(c):
+            for h in range(H):
+                bank = tp_pool.tile([P, BANK], F32, name="bank")
+                product(ax, wa, h, c, bank, nc.scalar.copy)
 
         ax = keep.tile([P, H, C], F32, name="ax")
-        for k in range(QUARTERS):
-            product(ax, wa, k)
         park = value_pool.tile([P, H, C], F32, name="vt")
         ux = keep.tile([P, H, C], F32, name="ux")
 
@@ -267,13 +274,17 @@ def tile_gnn_s2_pa_t_kernel(
             nc.vector.quantize_mx(out=eq[:].bitcast(FP8X4), scales=es[:], in_=groups[s][:])
             codes[s] = (eq, es)
 
+        def quarter(s, k):
+            return (k % 2, k // 2) if s == 0 else (k // 2, k % 2)
+
         def fill_message_bank(n):
             if n not in range(STEPS * QUARTERS):
                 return
             s, k = divmod(n, QUARTERS)
+            h, c = quarter(s, k)
             acc = mm_pool.tile([P, BANK], F32, name="acc")
-            mx_passes(acc, block_of(codes[s][0], codes[s][1], k // 2), we, columns(k), True, False)
-            mx_passes(acc, block_of(xr[:, s % Q, :], xrs[:, s % Q, :], k // 2), wb, columns(k), False, True)
+            mx_passes(acc, block_of(codes[s][0], codes[s][1], h), we, c, True, False)
+            mx_passes(acc, block_of(xr[:, s % Q, :], xrs[:, s % Q, :], h), wb, c, False, True)
             banks[n] = acc
 
         def evacuate(s, k):
@@ -281,23 +292,24 @@ def tile_gnn_s2_pa_t_kernel(
                 return
             if k == 0:
                 msgs[s] = msg_pool.tile([P, H, C], F32, name="msg")
+            h, c = quarter(s, k)
             nc.vector.scalar_tensor_tensor(
-                out=msgs[s][:, k // 2, columns(k)],
+                out=msgs[s][:, h, columns(c)],
                 in0=banks[QUARTERS * s + k][:],
                 scalar=1.0,
-                in1=ax[:, s // Q, columns(k)],
+                in1=ax[:, s // Q, columns(c)],
                 op0=ALU.mult,
                 op1=ALU.add,
-                accum_out=stats[:, s, 4 * (k // 2) + k % 2 : 4 * (k // 2) + k % 2 + 1],
+                accum_out=stats[:, s, 4 * h + c : 4 * h + c + 1],
             )
 
-        def early_products(t, k):
-            if t == 0:
-                product(park, wv, k)
-                if k == QUARTERS - 1:
-                    nc.sync.dma_start(out=out0_v, in_=flat(park))
-            if t == 2:
-                product(ux, wu, k)
+        def park_values(k):
+            if k not in range(QUARTERS):
+                return
+            acc = mm_pool.tile([P, BANK], F32, name="acc")
+            product(park, wv, k // 2, k % 2, acc, nc.scalar.copy)
+            if k == QUARTERS - 1:
+                nc.sync.dma_start(out=out0_v, in_=flat(park))
 
         def square_sum(rows, row, tile_index, parts):
             width = C // parts
@@ -449,28 +461,55 @@ def tile_gnn_s2_pa_t_kernel(
                     pieces_t[b] = t[:, cols]
             totals[label, half] = pieces_t
 
-        for t in range(-3, STEPS + 2):
-            if t >= 0:
-                load_edge(t + PREFETCH)
-            load_values(t - 1)
-            repeat_nodes(t + 2)
+        transpose_edge(0)
+        group_edge(0)
+        quantise_edge(0)
+        node_product(0)
+        repeat_nodes(0)
+        for n in range(MM_BANKS):
+            fill_message_bank(n)
+        node_product(1)
+        repeat_nodes(1)
+        load_edge(PREFETCH)
+        for k in (0, 1):
+            evacuate(0, k)
+            fill_message_bank(k + MM_BANKS)
+        transpose_edge(1)
+        group_edge(1)
+        for k in (2, 3):
+            evacuate(0, k)
+            park_values(k - 2)
+        quantise_edge(1)
+        for k in (2, 3):
+            fill_message_bank(k + MM_BANKS)
+        for h in range(H):
+            square_sum(msgs[0][:, h, :], 0, h, 1)
+        transpose_edge(2)
+        group_edge(2)
+        edge_sums(0)
+        repeat_nodes(2)
+        transpose_edge(3)
+        for t in range(1, STEPS):
+            load_edge(t + PREFETCH)
             for k in (0, 1):
                 evacuate(t, k)
-                early_products(t, k)
+                if t == 1:
+                    park_values(k + 2)
                 fill_message_bank(QUARTERS * t + k + MM_BANKS)
+            if t == 1:
+                edge_coefficients(0)
+                quantise_edge(2)
+            load_values(t - 1)
             weigh_values(t - 2, 0)
             sum_over_j("den", t - 2, gates.get(t - 2))
             finish_sums("den", t - 2)
-            if t in range(STEPS):
-                square_sum(msgs[t][:, 0, :], t, 0, 1)
+            square_sum(msgs[t][:, 0, :], t, 0, 1)
             for k in (2, 3):
                 evacuate(t, k)
-                early_products(t, k)
                 fill_message_bank(QUARTERS * t + k + MM_BANKS)
             weigh_values(t - 2, 1)
             group_edge(t + 2)
-            if t in range(STEPS):
-                square_sum(msgs[t][:, 1, :], t, 1, 1)
+            square_sum(msgs[t][:, 1, :], t, 1, 1)
             normalise(t - 1)
             finish_edge(t - 1)
             weights_of(t - 1)
@@ -480,17 +519,32 @@ def tile_gnn_s2_pa_t_kernel(
             transpose_edge(t + 3)
             edge_coefficients(t)
             quantise_edge(t + 2)
+            repeat_nodes(t + 2)
+        load_values(STEPS - 1)
+        for k in range(QUARTERS):
+            acc = mm_pool.tile([P, BANK], F32, name="acc")
+            product(ux, wu, k // 2, k % 2, acc, nc.vector.tensor_copy)
+        normalise(STEPS - 1)
+        finish_edge(STEPS - 1)
+        weights_of(STEPS - 1)
+        for s in (STEPS - 2, STEPS - 1):
+            for h in range(H):
+                weigh_values(s, h)
+            for label, tiles in (("den", gates), ("num", values)):
+                sum_over_j(label, s, tiles[s])
+                finish_sums(label, s)
 
         y = msg_pool.tile([P, H, C], F32, name="msg")
         act = gate_pool.tile([P, H, C], F32, name="gate")
         quo = keep.tile([P, H, C], F32, name="quo")
-        quarters = [(half, k, slice(k * BANK, (k + 1) * BANK)) for half in range(H) for k in range(C // BANK)]
-        for half, k, cols in quarters:
+        node_quarters = [(half, k, slice(k * BANK, (k + 1) * BANK)) for half in range(H) for k in range(C // BANK)]
+        for half, k, cols in node_quarters:
             nc.scalar.activation(
                 out=quo[:, half, cols], in_=totals["den", half][k], func=ACT.Abs_reciprocal_sqrt, scale=float(N)
             )
             nc.scalar.activation(out=quo[:, half, cols], in_=quo[:, half, cols], func=ACT.Square)
-        for half, k, cols in quarters:
+
+        def quotient_back(half, k, cols):
             nc.vector.tensor_tensor(
                 out=quo[:, half, cols], in0=totals["num", half][k], in1=quo[:, half, cols], op=ALU.mult
             )
@@ -501,6 +555,9 @@ def tile_gnn_s2_pa_t_kernel(
                     in_=quo[:, half, k * BANK + place * P : k * BANK + (place + 1) * P],
                     identity=ident[:],
                 )
+            return back
+
+        def node_sums(half, k, cols, back):
             nc.vector.scalar_tensor_tensor(
                 out=y[:, half, cols],
                 in0=back[:],
@@ -510,10 +567,20 @@ def tile_gnn_s2_pa_t_kernel(
                 op1=ALU.add,
                 accum_out=stats[:, STEPS, 4 * half + k : 4 * half + k + 1],
             )
-            if k == C // BANK - 1:
-                square_sum(y[:, half, :], STEPS, half, 2)
+            nc.scalar.activation(
+                out=act[:, half, cols],
+                in_=y[:, half, cols],
+                func=ACT.Square,
+                accum_out=stats[:, STEPS, 4 * half + 2 + k : 4 * half + 3 + k],
+            )
+
+        backs = [quotient_back(*node_quarters[0])]
+        for i, part in enumerate(node_quarters):
+            if i + 1 < len(node_quarters):
+                backs.append(quotient_back(*node_quarters[i + 1]))
+            node_sums(*part, backs[i])
         scale, offset = coefficients(moments_of(group_sums(STEPS)), slice(0, H), gain[:, 2 * STEPS :], shift[:, 2 * STEPS :])
-        for half, k, cols in quarters:
+        for half, k, cols in node_quarters:
             nc.scalar.activation(
                 out=act[:, half, cols],
                 in_=y[:, half, cols],

@@ -330,45 +330,74 @@ def tile_gnn_s2_pa_t_kernel(
             )
             return sums
 
-        def moments_of(sums):
-            moments = small_pool.tile([P, 2, H], F32, name="moments")
-            nc.vector.tensor_reduce(
-                out=moments[:], in_=sums[:].rearrange("p (h k t) -> p k h t", k=2, t=2), axis=AX.X, op=ALU.add
-            )
-            return moments
-
-        def coefficients(moments, col, gains, shifts):
-            mean, square = moments[:, 0, col], moments[:, 1, col]
-            width = col.stop - col.start
-            sq_mean = small_pool.tile([P, H], F32, name="sq_mean")
-            nc.gpsimd.tensor_tensor(out=sq_mean[:, 0:width], in0=mean, in1=mean, op=ALU.mult)
-            var = small_pool.tile([P, H], F32, name="var")
-            nc.gpsimd.tensor_tensor(out=var[:, 0:width], in0=square, in1=sq_mean[:, 0:width], op=ALU.subtract)
-            safe = small_pool.tile([P, H], F32, name="safe")
-            nc.gpsimd.tensor_scalar(
-                out=safe[:, 0:width], in0=var[:, 0:width], scalar1=0.0, scalar2=EPS, op0=ALU.max, op1=ALU.add
-            )
-            rstd = small_pool.tile([P, H], F32, name="rstd")
-            nc.gpsimd.tensor_tensor(out=rstd[:, 0:width], in0=safe[:, 0:width], in1=minus_half[:, 0:width], op=ALU.pow)
-            scale = small_pool.tile([P, H], F32, name="scale")
-            nc.gpsimd.tensor_tensor(out=scale[:, 0:width], in0=rstd[:, 0:width], in1=gains, op=ALU.mult)
-            drift = small_pool.tile([P, H], F32, name="drift")
-            nc.gpsimd.tensor_tensor(out=drift[:, 0:width], in0=mean, in1=scale[:, 0:width], op=ALU.mult)
-            offset = small_pool.tile([P, H], F32, name="offset")
-            nc.gpsimd.tensor_tensor(out=offset[:, 0:width], in0=shifts, in1=drift[:, 0:width], op=ALU.subtract)
-            return scale, offset
-
         sums_of = {}
+        moments = {}
+        small = {}
 
         def edge_sums(s):
             if s in range(STEPS):
                 sums_of[s] = group_sums(s)
 
-        def edge_coefficients(s):
-            if s not in range(STEPS):
+        def take_moments(s):
+            if s not in range(STEPS + 1):
                 return
-            cols = slice(H * s, H * s + H)
-            coeffs[s] = coefficients(moments_of(sums_of[s]), slice(0, H), gain[:, cols], shift[:, cols])
+            moments[s] = small_pool.tile([P, 2, H], F32, name="moments")
+            nc.vector.tensor_reduce(
+                out=moments[s][:], in_=sums_of[s][:].rearrange("p (h k t) -> p k h t", k=2, t=2), axis=AX.X, op=ALU.add
+            )
+
+        def square_means(s):
+            if s not in range(STEPS + 1):
+                return
+            small[s, "square"] = small_pool.tile([P, H], F32, name="sq_mean")
+            nc.vector.tensor_tensor(
+                out=small[s, "square"][:], in0=moments[s][:, 0], in1=moments[s][:, 0], op=ALU.mult
+            )
+
+        def variances(s):
+            if s not in range(STEPS + 1):
+                return
+            small[s, "var"] = small_pool.tile([P, H], F32, name="var")
+            nc.vector.tensor_tensor(
+                out=small[s, "var"][:], in0=moments[s][:, 1], in1=small[s, "square"][:], op=ALU.subtract
+            )
+
+        def deviations(s):
+            if s not in range(STEPS + 1):
+                return
+            safe = small_pool.tile([P, H], F32, name="safe")
+            nc.vector.tensor_scalar(
+                out=safe[:], in0=small[s, "var"][:], scalar1=0.0, scalar2=EPS, op0=ALU.max, op1=ALU.add
+            )
+            small[s, "rstd"] = small_pool.tile([P, H], F32, name="rstd")
+            nc.gpsimd.tensor_tensor(out=small[s, "rstd"][:], in0=safe[:], in1=minus_half[:], op=ALU.pow)
+
+        def scales(s):
+            if s not in range(STEPS + 1):
+                return
+            small[s, "scale"] = small_pool.tile([P, H], F32, name="scale")
+            nc.vector.tensor_tensor(
+                out=small[s, "scale"][:], in0=small[s, "rstd"][:], in1=gain[:, H * s : H * s + H], op=ALU.mult
+            )
+
+        def drifts(s):
+            if s not in range(STEPS + 1):
+                return
+            small[s, "drift"] = small_pool.tile([P, H], F32, name="drift")
+            nc.vector.tensor_tensor(
+                out=small[s, "drift"][:], in0=moments[s][:, 0], in1=small[s, "scale"][:], op=ALU.mult
+            )
+
+        def offsets(s):
+            if s not in range(STEPS + 1):
+                return
+            offset = small_pool.tile([P, H], F32, name="offset")
+            nc.vector.tensor_tensor(
+                out=offset[:], in0=shift[:, H * s : H * s + H], in1=small[s, "drift"][:], op=ALU.subtract
+            )
+            coeffs[s] = (small[s, "scale"], offset)
+
+        chain = (square_means, variances, deviations, scales, drifts, offsets)
 
         def normalise(s):
             if s not in range(STEPS):
@@ -388,10 +417,14 @@ def tile_gnn_s2_pa_t_kernel(
             count = QUARTERS if s == STEPS - 1 else H
             return [slice(i * W // count, (i + 1) * W // count) for i in range(count)]
 
-        def finish_edge(s):
+        def half_pieces(s, h):
+            cols = pieces(s)
+            return cols[h * len(cols) // H : (h + 1) * len(cols) // H]
+
+        def finish_edge(s, h):
             if s not in range(STEPS):
                 return
-            for cols in pieces(s):
+            for cols in half_pieces(s, h):
                 nc.vector.scalar_tensor_tensor(
                     out=flat(msgs[s])[:, cols],
                     in0=flat(msgs[s])[:, cols],
@@ -400,6 +433,8 @@ def tile_gnn_s2_pa_t_kernel(
                     op0=ALU.max,
                     op1=ALU.add,
                 )
+            if h < H - 1:
+                return
             q = s % Q
             nc.sync.dma_start(out=out1_v[:, s // Q, q * W : (q + 1) * W], in_=flat(msgs[s]))
 
@@ -419,10 +454,11 @@ def tile_gnn_s2_pa_t_kernel(
             nc.sync.dma_start(out=flat(vt), in_=parked_v[:, s % Q, :].unsqueeze(1).to_broadcast([N, Q, W]))
             values[s] = vt
 
-        def weigh_values(s, h):
+        def weigh_values(s, h, parts=1, part=0):
             if s not in range(STEPS):
                 return
-            for cols in pieces(s)[h * len(pieces(s)) // H : (h + 1) * len(pieces(s)) // H]:
+            width = C // parts
+            for cols in (half_pieces(s, h) if parts == 1 else [slice(h * C + part * width, h * C + (part + 1) * width)]):
                 nc.vector.tensor_tensor(
                     out=flat(values[s])[:, cols], in0=flat(values[s])[:, cols], in1=flat(gates[s])[:, cols], op=ALU.mult
                 )
@@ -487,18 +523,23 @@ def tile_gnn_s2_pa_t_kernel(
         transpose_edge(2)
         group_edge(2)
         edge_sums(0)
-        repeat_nodes(2)
         transpose_edge(3)
         for t in range(1, STEPS):
             load_edge(t + PREFETCH)
-            for k in (0, 1):
-                evacuate(t, k)
-                if t == 1:
-                    park_values(k + 2)
-                fill_message_bank(QUARTERS * t + k + MM_BANKS)
+            take_moments(t - 1)
+            evacuate(t, 0)
             if t == 1:
-                edge_coefficients(0)
-                quantise_edge(2)
+                park_values(2)
+            fill_message_bank(QUARTERS * t + MM_BANKS)
+            square_means(t - 1)
+            evacuate(t, 1)
+            if t == 1:
+                park_values(3)
+            fill_message_bank(QUARTERS * t + 1 + MM_BANKS)
+            variances(t - 1)
+            quantise_edge(t + 1)
+            repeat_nodes(t + 1)
+            deviations(t - 1)
             load_values(t - 1)
             weigh_values(t - 2, 0)
             sum_over_j("den", t - 2, gates.get(t - 2))
@@ -507,25 +548,31 @@ def tile_gnn_s2_pa_t_kernel(
             for k in (2, 3):
                 evacuate(t, k)
                 fill_message_bank(QUARTERS * t + k + MM_BANKS)
-            weigh_values(t - 2, 1)
+            scales(t - 1)
+            weigh_values(t - 2, 1, 2, 0)
+            drifts(t - 1)
+            weigh_values(t - 2, 1, 2, 1)
             group_edge(t + 2)
             square_sum(msgs[t][:, 1, :], t, 1, 1)
+            offsets(t - 1)
             normalise(t - 1)
-            finish_edge(t - 1)
-            weights_of(t - 1)
             sum_over_j("num", t - 2, values.get(t - 2))
             finish_sums("num", t - 2)
             edge_sums(t)
             transpose_edge(t + 3)
-            edge_coefficients(t)
-            quantise_edge(t + 2)
-            repeat_nodes(t + 2)
+            finish_edge(t - 1, 0)
+            finish_edge(t - 1, 1)
+            weights_of(t - 1)
         load_values(STEPS - 1)
-        for k in range(QUARTERS):
-            acc = mm_pool.tile([P, BANK], F32, name="acc")
-            product(ux, wu, k // 2, k % 2, acc, nc.vector.tensor_copy)
+        take_moments(STEPS - 1)
+        for k, stage in enumerate(chain):
+            stage(STEPS - 1)
+            if k < QUARTERS:
+                acc = mm_pool.tile([P, BANK], F32, name="acc")
+                product(ux, wu, k // 2, k % 2, acc, nc.vector.tensor_copy)
         normalise(STEPS - 1)
-        finish_edge(STEPS - 1)
+        for h in range(H):
+            finish_edge(STEPS - 1, h)
         weights_of(STEPS - 1)
         for s in (STEPS - 2, STEPS - 1):
             for h in range(H):
@@ -579,7 +626,11 @@ def tile_gnn_s2_pa_t_kernel(
             if i + 1 < len(node_quarters):
                 backs.append(quotient_back(*node_quarters[i + 1]))
             node_sums(*part, backs[i])
-        scale, offset = coefficients(moments_of(group_sums(STEPS)), slice(0, H), gain[:, 2 * STEPS :], shift[:, 2 * STEPS :])
+        sums_of[STEPS] = group_sums(STEPS)
+        take_moments(STEPS)
+        for stage in chain:
+            stage(STEPS)
+        scale, offset = coeffs[STEPS]
         for half, k, cols in node_quarters:
             nc.scalar.activation(
                 out=act[:, half, cols],

@@ -65,9 +65,9 @@ def tile_gnn_s2_pa_t_kernel(
         edge_pool = ctx.enter_context(tc.tile_pool(name="edge", bufs=PREFETCH + 2))
         group_pool = ctx.enter_context(tc.tile_pool(name="group", bufs=2))
         code_pool = ctx.enter_context(tc.tile_pool(name="code", bufs=3))
-        msg_pool = ctx.enter_context(tc.tile_pool(name="msg", bufs=3))
+        msg_pool = ctx.enter_context(tc.tile_pool(name="msg", bufs=4))
         gate_pool = ctx.enter_context(tc.tile_pool(name="gate", bufs=2))
-        value_pool = ctx.enter_context(tc.tile_pool(name="value", bufs=3))
+        value_pool = ctx.enter_context(tc.tile_pool(name="value", bufs=4))
         junk_pool = ctx.enter_context(tc.tile_pool(name="junk", bufs=1))
         small_pool = ctx.enter_context(tc.tile_pool(name="small", bufs=3))
         tp_pool = ctx.enter_context(tc.psum_pool(name="tp", bufs=2))
@@ -229,10 +229,10 @@ def tile_gnn_s2_pa_t_kernel(
             mx_passes(acc, block_of(xq, xs, h), weights, c, True, True)
             copy(out=dst[:, h, columns(c)], in_=acc[:])
 
-        def node_product(c):
+        def node_product(dst, weights, c, copy):
             for h in range(H):
                 bank = tp_pool.tile([P, BANK], F32, name="bank")
-                product(ax, wa, h, c, bank, nc.scalar.copy)
+                product(dst, weights, h, c, bank, copy)
 
         ax = keep.tile([P, H, C], F32, name="ax")
         park = value_pool.tile([P, H, C], F32, name="vt")
@@ -303,12 +303,9 @@ def tile_gnn_s2_pa_t_kernel(
                 accum_out=stats[:, s, 4 * h + c : 4 * h + c + 1],
             )
 
-        def park_values(k):
-            if k not in range(QUARTERS):
-                return
-            acc = mm_pool.tile([P, BANK], F32, name="acc")
-            product(park, wv, k // 2, k % 2, acc, nc.scalar.copy)
-            if k == QUARTERS - 1:
+        def park_values(c):
+            node_product(park, wv, c, nc.scalar.copy)
+            if c == 1:
                 nc.sync.dma_start(out=out0_v, in_=flat(park))
 
         def square_sum(rows, row, tile_index, parts):
@@ -397,21 +394,23 @@ def tile_gnn_s2_pa_t_kernel(
             )
             coeffs[s] = (small[s, "scale"], offset)
 
-        chain = (square_means, variances, deviations, scales, drifts, offsets)
-
-        def normalise(s):
+        def normalise(s, h):
             if s not in range(STEPS):
                 return
             scale, offset = coeffs[s]
+            nc.vector.tensor_scalar(
+                out=msgs[s][:, h, :],
+                in0=msgs[s][:, h, :],
+                scalar1=scale[:, h : h + 1],
+                scalar2=offset[:, h : h + 1],
+                op0=ALU.mult,
+                op1=ALU.add,
+            )
+
+        def node_sum_terms(c):
             for h in range(H):
-                nc.vector.tensor_scalar(
-                    out=msgs[s][:, h, :],
-                    in0=msgs[s][:, h, :],
-                    scalar1=scale[:, h : h + 1],
-                    scalar2=offset[:, h : h + 1],
-                    op0=ALU.mult,
-                    op1=ALU.add,
-                )
+                acc = mm_pool.tile([P, BANK], F32, name="acc")
+                product(ux, wu, h, c, acc, nc.vector.tensor_copy)
 
         def pieces(s):
             count = QUARTERS if s == STEPS - 1 else H
@@ -500,11 +499,11 @@ def tile_gnn_s2_pa_t_kernel(
         transpose_edge(0)
         group_edge(0)
         quantise_edge(0)
-        node_product(0)
+        node_product(ax, wa, 0, nc.scalar.copy)
         repeat_nodes(0)
         for n in range(MM_BANKS):
             fill_message_bank(n)
-        node_product(1)
+        node_product(ax, wa, 1, nc.scalar.copy)
         repeat_nodes(1)
         load_edge(PREFETCH)
         for k in (0, 1):
@@ -514,40 +513,65 @@ def tile_gnn_s2_pa_t_kernel(
         group_edge(1)
         for k in (2, 3):
             evacuate(0, k)
-            park_values(k - 2)
+        park_values(0)
         quantise_edge(1)
         for k in (2, 3):
             fill_message_bank(k + MM_BANKS)
+        load_edge(1 + PREFETCH)
+        for k in (0, 1):
+            evacuate(1, k)
+            fill_message_bank(QUARTERS + k + MM_BANKS)
         for h in range(H):
             square_sum(msgs[0][:, h, :], 0, h, 1)
+        park_values(1)
         transpose_edge(2)
         group_edge(2)
         edge_sums(0)
+        for k in (2, 3):
+            evacuate(1, k)
+        take_moments(0)
+        repeat_nodes(2)
+        square_means(0)
+        quantise_edge(2)
+        variances(0)
+        load_values(0)
+        load_values(1)
+        for k in (2, 3):
+            fill_message_bank(QUARTERS + k + MM_BANKS)
+        for h in range(H):
+            square_sum(msgs[1][:, h, :], 1, h, 1)
+        deviations(0)
+        scales(0)
         transpose_edge(3)
-        for t in range(1, STEPS):
+        group_edge(3)
+        drifts(0)
+        edge_sums(1)
+        offsets(0)
+        for h in range(H):
+            normalise(0, h)
+            finish_edge(0, h)
+        weights_of(0)
+        transpose_edge(4)
+        for t in range(2, STEPS):
             load_edge(t + PREFETCH)
             take_moments(t - 1)
             evacuate(t, 0)
-            if t == 1:
-                park_values(2)
             fill_message_bank(QUARTERS * t + MM_BANKS)
             square_means(t - 1)
             evacuate(t, 1)
-            if t == 1:
-                park_values(3)
             fill_message_bank(QUARTERS * t + 1 + MM_BANKS)
             variances(t - 1)
             quantise_edge(t + 1)
             repeat_nodes(t + 1)
             deviations(t - 1)
-            load_values(t - 1)
+            load_values(t)
             weigh_values(t - 2, 0)
             sum_over_j("den", t - 2, gates.get(t - 2))
             finish_sums("den", t - 2)
             square_sum(msgs[t][:, 0, :], t, 0, 1)
             for k in (2, 3):
                 evacuate(t, k)
-                fill_message_bank(QUARTERS * t + k + MM_BANKS)
+            fill_message_bank(QUARTERS * t + 2 + MM_BANKS)
             scales(t - 1)
             weigh_values(t - 2, 1, 2, 0)
             drifts(t - 1)
@@ -555,28 +579,33 @@ def tile_gnn_s2_pa_t_kernel(
             group_edge(t + 2)
             square_sum(msgs[t][:, 1, :], t, 1, 1)
             offsets(t - 1)
-            normalise(t - 1)
+            for h in range(H):
+                normalise(t - 1, h)
             sum_over_j("num", t - 2, values.get(t - 2))
             finish_sums("num", t - 2)
+            fill_message_bank(QUARTERS * t + 3 + MM_BANKS)
             edge_sums(t)
             transpose_edge(t + 3)
             finish_edge(t - 1, 0)
             finish_edge(t - 1, 1)
             weights_of(t - 1)
-        load_values(STEPS - 1)
         take_moments(STEPS - 1)
-        for k, stage in enumerate(chain):
-            stage(STEPS - 1)
-            if k < QUARTERS:
-                acc = mm_pool.tile([P, BANK], F32, name="acc")
-                product(ux, wu, k // 2, k % 2, acc, nc.vector.tensor_copy)
-        normalise(STEPS - 1)
+        square_means(STEPS - 1)
+        variances(STEPS - 1)
+        deviations(STEPS - 1)
+        node_sum_terms(0)
+        scales(STEPS - 1)
+        drifts(STEPS - 1)
+        offsets(STEPS - 1)
         for h in range(H):
+            normalise(STEPS - 1, h)
             finish_edge(STEPS - 1, h)
         weights_of(STEPS - 1)
         for s in (STEPS - 2, STEPS - 1):
             for h in range(H):
                 weigh_values(s, h)
+            if s == STEPS - 2:
+                node_sum_terms(1)
             for label, tiles in (("den", gates), ("num", values)):
                 sum_over_j(label, s, tiles[s])
                 finish_sums(label, s)
@@ -628,8 +657,15 @@ def tile_gnn_s2_pa_t_kernel(
             node_sums(*part, backs[i])
         sums_of[STEPS] = group_sums(STEPS)
         take_moments(STEPS)
-        for stage in chain:
-            stage(STEPS)
+        square_means(STEPS)
+        variances(STEPS)
+        small[STEPS, "rstd"] = small_pool.tile([P, H], F32, name="rstd")
+        nc.scalar.activation(
+            out=small[STEPS, "rstd"][:], in_=small[STEPS, "var"][:], func=ACT.Abs_reciprocal_sqrt, bias=EPS
+        )
+        scales(STEPS)
+        drifts(STEPS)
+        offsets(STEPS)
         scale, offset = coeffs[STEPS]
         for half, k, cols in node_quarters:
             nc.scalar.activation(

@@ -27,6 +27,7 @@ EPS = 1e-5
 COUNT = 16 * C
 
 MM_BANKS = 2
+SCALAR_COLS = 512
 PREFETCH = 4
 
 FLOPS = 2 * C * C * (16 * 256 + 4 * 16 * 16)
@@ -191,8 +192,6 @@ def tile_gnn_s2_pa_t_kernel(
         xs4_v = xs4[:].bitcast(I32).rearrange("p (a q) -> p q a", q=Q)
 
         def repeat_nodes(q):
-            if q not in range(Q):
-                return
             nc.vector.tensor_copy(
                 out=xr[:, q, :].rearrange("p (a i) -> p a i", i=Q),
                 in_=xq_v[:, q].unsqueeze(2).to_broadcast([P, G * H * N, Q]),
@@ -398,14 +397,24 @@ def tile_gnn_s2_pa_t_kernel(
             if s not in range(STEPS):
                 return
             scale, offset = coeffs[s]
+            shared = h == H - 1 and s not in (0, Q + 1)
+            width = C - SCALAR_COLS if shared else C
             nc.vector.tensor_scalar(
-                out=msgs[s][:, h, :],
-                in0=msgs[s][:, h, :],
+                out=msgs[s][:, h, :width],
+                in0=msgs[s][:, h, :width],
                 scalar1=scale[:, h : h + 1],
                 scalar2=offset[:, h : h + 1],
                 op0=ALU.mult,
                 op1=ALU.add,
             )
+            if width < C:
+                nc.scalar.activation(
+                    out=msgs[s][:, h, width:],
+                    in_=msgs[s][:, h, width:],
+                    func=ACT.Identity,
+                    scale=scale[:, h : h + 1],
+                    bias=offset[:, h : h + 1],
+                )
 
         def node_sum_terms(c):
             for h in range(H):
@@ -504,15 +513,18 @@ def tile_gnn_s2_pa_t_kernel(
         for n in range(MM_BANKS):
             fill_message_bank(n)
         node_product(ax, wa, 1, nc.scalar.copy)
-        repeat_nodes(1)
         load_edge(PREFETCH)
         for k in (0, 1):
             evacuate(0, k)
             fill_message_bank(k + MM_BANKS)
         transpose_edge(1)
         group_edge(1)
+        for q in (1, 2, 3):
+            repeat_nodes(q)
         for k in (2, 3):
             evacuate(0, k)
+        for q in (4, 5, 6):
+            repeat_nodes(q)
         park_values(0)
         quantise_edge(1)
         for k in (2, 3):
@@ -529,8 +541,8 @@ def tile_gnn_s2_pa_t_kernel(
         edge_sums(0)
         for k in (2, 3):
             evacuate(1, k)
+        repeat_nodes(7)
         take_moments(0)
-        repeat_nodes(2)
         square_means(0)
         quantise_edge(2)
         variances(0)
@@ -562,12 +574,10 @@ def tile_gnn_s2_pa_t_kernel(
             fill_message_bank(QUARTERS * t + 1 + MM_BANKS)
             variances(t - 1)
             quantise_edge(t + 1)
-            repeat_nodes(t + 1)
             deviations(t - 1)
             load_values(t)
             weigh_values(t - 2, 0)
             sum_over_j("den", t - 2, gates.get(t - 2))
-            finish_sums("den", t - 2)
             square_sum(msgs[t][:, 0, :], t, 0, 1)
             for k in (2, 3):
                 evacuate(t, k)
@@ -582,13 +592,14 @@ def tile_gnn_s2_pa_t_kernel(
             for h in range(H):
                 normalise(t - 1, h)
             sum_over_j("num", t - 2, values.get(t - 2))
-            finish_sums("num", t - 2)
             fill_message_bank(QUARTERS * t + 3 + MM_BANKS)
             edge_sums(t)
             transpose_edge(t + 3)
             finish_edge(t - 1, 0)
             finish_edge(t - 1, 1)
             weights_of(t - 1)
+            for label in ("den", "num"):
+                finish_sums(label, t - 2)
         take_moments(STEPS - 1)
         square_means(STEPS - 1)
         variances(STEPS - 1)

from contextlib import ExitStack

import concourse.mybir as mybir
from concourse.masks import make_identity

F32 = mybir.dt.float32
BF16 = mybir.dt.bfloat16
I32 = mybir.dt.int32
U8 = mybir.dt.uint8
FP8X4 = mybir.dt.float8_e4m3fn_x4
ALU = mybir.AluOpType
ACT = mybir.ActivationFunctionType
AX = mybir.AxisListType

P = 128
N = 16
C = 1024
H = 2
Q = 8
W = H * C
G = 2
BANK = 512
QUARTERS = W // BANK
STEPS = H * Q
CHUNKS = C // P
EPS = 1e-5
COUNT = 16 * C

MM_BANKS = 2
SCALAR_COLS = 512
PREFETCH = 4

FLOPS = 2 * C * C * (16 * 256 + 4 * 16 * 16)


def tile_gnn_s2_pa_t_kernel(
    tc,
    x,
    edge,
    Wu_words,
    Wu_scales,
    Wv_words,
    Wv_scales,
    Wa_words,
    Wa_scales,
    Wb_words,
    Wb_scales,
    We_words,
    We_scales,
    bnv_w,
    bnv_b,
    bne_w,
    bne_b,
    out_0,
    out_1,
):
    nc = tc.nc
    edge_v = edge.rearrange("b (q h j) c -> (b q) h (j c)", q=Q, h=H)
    out1_v = out_1.rearrange("b (q h j) c -> (b q) h (j c)", q=Q, h=H)
    out0_v = out_0.rearrange("b (q h) c -> (b q) (h c)", q=Q, h=H)
    parked_v = out_0.rearrange("b (q h) c -> b q (h c)", q=Q, h=H)

    with ExitStack() as ctx:
        ctx.enter_context(tc.manual_schedule())
        keep = ctx.enter_context(tc.tile_pool(name="keep", bufs=1))
        edge_pool = ctx.enter_context(tc.tile_pool(name="edge", bufs=PREFETCH + 2))
        group_pool = ctx.enter_context(tc.tile_pool(name="group", bufs=2))
        code_pool = ctx.enter_context(tc.tile_pool(name="code", bufs=3))
        msg_pool = ctx.enter_context(tc.tile_pool(name="msg", bufs=4))
        gate_pool = ctx.enter_context(tc.tile_pool(name="gate", bufs=2))
        value_pool = ctx.enter_context(tc.tile_pool(name="value", bufs=4))
        junk_pool = ctx.enter_context(tc.tile_pool(name="junk", bufs=1))
        small_pool = ctx.enter_context(tc.tile_pool(name="small", bufs=3))
        tp_pool = ctx.enter_context(tc.psum_pool(name="tp", bufs=2))
        mm_pool = ctx.enter_context(tc.psum_pool(name="mm", bufs=MM_BANKS))
        acc_pool = ctx.enter_context(tc.psum_pool(name="sum", bufs=1))

        def start_weight(scales, label):
            halves = [keep.tile([P, G, BANK], I32, name=label + "_codes" + str(c), align_bytes=64) for c in range(2)]
            plane = keep.tile([P, G, C], U8, name=label + "_plane", align_bytes=64)
            nc.vector.memset(plane[:].rearrange("p g n -> p (g n)").bitcast(I32), 0)
            for quad in range(4):
                nc.sync.dma_start(
                    out=plane[32 * quad : 32 * quad + 4, :, :].bitcast(I32),
                    in_=scales[:, 4 * quad : 4 * quad + 4, :].rearrange("g r n -> r g n").bitcast(I32),
                )
            return halves, plane

        def load_codes(weight, words, c):
            nc.sync.dma_start(
                out=weight[0][c][:],
                in_=words[:, :, c * BANK : (c + 1) * BANK, :].rearrange("g p n t -> p g (n t)").bitcast(I32),
            )

        edge_tiles = {}

        def load_edge(s):
            if s not in range(STEPS):
                return
            h, q = divmod(s, Q)
            et = edge_pool.tile([P, H, C], BF16, name="et")
            nc.sync.dma_start(out=flat(et), in_=edge_v[:, h, q * W : (q + 1) * W])
            edge_tiles[s] = et

        def flat(t):
            return t[:].rearrange("p h c -> p (h c)")

        params = []
        for by_edge, by_node, label in ((bne_w, bnv_w, "w"), (bne_b, bnv_b, "b")):
            e_bf = keep.tile([P, 2 * STEPS], BF16, name="bne_" + label)
            v_bf = keep.tile([P, H], BF16, name="bnv_" + label)
            nc.scalar.dma_start(
                out=e_bf[:], in_=by_edge.rearrange("(q r) -> q r", q=Q).unsqueeze(0).to_broadcast([N, Q, 2 * STEPS])
            )
            nc.scalar.dma_start(
                out=v_bf[:], in_=by_node.rearrange("(q h) -> q h", q=Q).unsqueeze(0).to_broadcast([N, Q, H])
            )
            params.append((e_bf, v_bf))

        warm = keep.tile([P, 1], F32, name="warm")
        nc.vector.memset(warm[:], 0.0)
        nc.scalar.activation(out=warm[:], in_=warm[:], func=ACT.Tanh)

        x_sb = keep.tile([P, H, C], BF16, name="x_sb")
        nc.sync.dma_start(out=flat(x_sb), in_=x.rearrange("b (q h) c -> (b q) (h c)", q=Q, h=H))
        load_edge(0)
        wa = start_weight(Wa_scales, "wa")
        we = start_weight(We_scales, "we")
        wb = start_weight(Wb_scales, "wb")
        for c in range(2):
            load_codes(wa, Wa_words, c)
            load_codes(we, We_words, c)
            load_codes(wb, Wb_words, c)
        load_edge(1)
        load_edge(2)
        wv = start_weight(Wv_scales, "wv")
        for c in range(2):
            load_codes(wv, Wv_words, c)
        for s in range(3, PREFETCH):
            load_edge(s)
        wu = start_weight(Wu_scales, "wu")
        for c in range(2):
            load_codes(wu, Wu_words, c)

        ident = keep.tile([P, P], F32, name="ident")
        make_identity(nc, ident[:])
        same_i = keep.tile([P, Q], F32, name="same_i")
        nc.vector.tensor_reduce(
            out=same_i[:], in_=ident[:].rearrange("p (b q) -> p q b", q=Q), axis=AX.X, op=ALU.add
        )
        group_mean = keep.tile([P, N, Q], F32, name="group_mean")
        nc.vector.tensor_scalar_mul(
            out=group_mean[:], in0=same_i[:].unsqueeze(1).to_broadcast([P, N, Q]), scalar1=1.0 / COUNT
        )
        minus_half = keep.tile([P, H], F32, name="minus_half")
        nc.vector.memset(minus_half[:], -0.5)
        stats = keep.tile([P, STEPS + 1, H * 4], F32, name="stats")
        nc.vector.memset(stats[:], 0.0)

        def transpose_words(bank, rows):
            words = rows.bitcast(F32)
            for g in range(G):
                for u in range(2):
                    nc.tensor.transpose(
                        out=bank[:, g, u, :], in_=words[:, 256 * g + u : 256 * (g + 1) : 2], identity=ident[:]
                    )

        xg = keep.tile([P, G * H * P * 4], BF16, name="xg", align_bytes=64)
        xg_words = xg[:].bitcast(F32).rearrange("p (g h r u) -> p g h r u", g=G, h=H, u=2)
        xs4 = keep.tile([P, G * H * P * 4], U8, name="xs4", align_bytes=64)
        for h in range(H):
            bank = tp_pool.tile([P, G, 2, P], F32, name="bank")
            transpose_words(bank, x_sb[:, h, :])
            nc.vector.tensor_copy(out=xg_words[:, :, h], in_=bank[:].rearrange("p g u r -> p g r u"))
        xq = keep.tile([P, G * H * P], I32, name="xq", align_bytes=64)
        xs = keep.tile([P, G * H * P], U8, name="xs", align_bytes=64)
        nc.vector.memset(xs[:].bitcast(I32), 0)
        nc.vector.quantize_mx(out=xq[:].bitcast(FP8X4), scales=xs[:], in_=xg[:])
        xs4_bytes = xs4[:].rearrange("p (a f) -> p a f", f=4)
        for copy in range(4):
            nc.vector.tensor_copy(out=xs4_bytes[:, :, copy], in_=xs[:])

        gain = keep.tile([P, 2 * STEPS + H], F32, name="gain")
        shift = keep.tile([P, 2 * STEPS + H], F32, name="shift")
        for dst, (e_bf, v_bf) in zip((gain, shift), params):
            nc.vector.tensor_copy(out=dst[:, 0 : 2 * STEPS], in_=e_bf[:])
            nc.vector.tensor_copy(out=dst[:, 2 * STEPS :], in_=v_bf[:])

        xr = keep.tile([P, Q, G * H * P], I32, name="xr", align_bytes=64)
        xrs = keep.tile([P, Q, G * H * P], U8, name="xrs", align_bytes=64)
        xq_v = xq[:].rearrange("p (a q) -> p q a", q=Q)
        xs4_v = xs4[:].bitcast(I32).rearrange("p (a q) -> p q a", q=Q)

        def repeat_nodes(q):
            nc.vector.tensor_copy(
                out=xr[:, q, :].rearrange("p (a i) -> p a i", i=Q),
                in_=xq_v[:, q].unsqueeze(2).to_broadcast([P, G * H * N, Q]),
            )
            nc.vector.tensor_copy(
                out=xrs[:, q, :].bitcast(I32).rearrange("p (a w) -> p a w", w=2),
                in_=xs4_v[:, q].unsqueeze(2).to_broadcast([P, G * H * N, 2]),
            )

        def mx_passes(acc, stationary, weights, c, first, last):
            s_codes, s_plane = stationary
            w_codes, w_plane = weights
            for g in range(G):
                nc.tensor.matmul_mx(
                    out=acc[:],
                    lhsT=s_codes(g).bitcast(FP8X4),
                    lhsT_scale=s_plane(g),
                    rhs=w_codes[c][:, g, :].bitcast(FP8X4),
                    rhs_scale=w_plane[:, g, columns(c)],
                    start=first and g == 0,
                    stop=last and g == G - 1,
                )

        def block_of(codes, plane, h):
            def cut(t):
                return lambda g: t[:, (g * H + h) * P : (g * H + h + 1) * P]

            return cut(codes), cut(plane)

        def columns(k):
            return slice((k % 2) * BANK, (k % 2 + 1) * BANK)

        def product(dst, weights, h, c, acc, copy):
            mx_passes(acc, block_of(xq, xs, h), weights, c, True, True)
            copy(out=dst[:, h, columns(c)], in_=acc[:])

        def node_product(dst, weights, c, copy):
            for h in range(H):
                bank = tp_pool.tile([P, BANK], F32, name="bank")
                product(dst, weights, h, c, bank, copy)

        ax = keep.tile([P, H, C], F32, name="ax")
        park = value_pool.tile([P, H, C], F32, name="vt")
        ux = keep.tile([P, H, C], F32, name="ux")

        flipped = {}
        groups = {}
        codes = {}
        banks = {}
        msgs = {}
        gates = {}
        values = {}
        coeffs = {}
        totals = {}
        sums_t = {}

        def transpose_edge(s):
            if s not in range(STEPS):
                return
            for h in range(H):
                bank = tp_pool.tile([P, G, 2, P], F32, name="bank")
                transpose_words(bank, edge_tiles[s][:, h, :])
                flipped[s, h] = bank

        def group_edge(s):
            if s not in range(STEPS):
                return
            eg = group_pool.tile([P, G * H * P * 4], BF16, name="eg", align_bytes=64)
            eg_words = eg[:].bitcast(F32).rearrange("p (g h r u) -> p g h r u", g=G, h=H, u=2)
            for h in range(H):
                nc.scalar.copy(out=eg_words[:, :, h], in_=flipped[s, h][:].rearrange("p g u r -> p g r u"))
            groups[s] = eg

        def quantise_edge(s):
            if s not in range(STEPS):
                return
            eq = code_pool.tile([P, G * H * P], I32, name="eq", align_bytes=64)
            es = code_pool.tile([P, G * H * P], U8, name="es", align_bytes=64)
            nc.vector.quantize_mx(out=eq[:].bitcast(FP8X4), scales=es[:], in_=groups[s][:])
            codes[s] = (eq, es)

        def quarter(s, k):
            return (k % 2, k // 2) if s == 0 else (k // 2, k % 2)

        def fill_message_bank(n):
            if n not in range(STEPS * QUARTERS):
                return
            s, k = divmod(n, QUARTERS)
            h, c = quarter(s, k)
            acc = mm_pool.tile([P, BANK], F32, name="acc")
            mx_passes(acc, block_of(codes[s][0], codes[s][1], h), we, c, True, False)
            mx_passes(acc, block_of(xr[:, s % Q, :], xrs[:, s % Q, :], h), wb, c, False, True)
            banks[n] = acc

        def evacuate(s, k):
            if s not in range(STEPS):
                return
            if k == 0:
                msgs[s] = msg_pool.tile([P, H, C], F32, name="msg")
            h, c = quarter(s, k)
            nc.vector.scalar_tensor_tensor(
                out=msgs[s][:, h, columns(c)],
                in0=banks[QUARTERS * s + k][:],
                scalar=1.0,
                in1=ax[:, s // Q, columns(c)],
                op0=ALU.mult,
                op1=ALU.add,
                accum_out=stats[:, s, 4 * h + c : 4 * h + c + 1],
            )

        def park_values(c):
            node_product(park, wv, c, nc.scalar.copy)
            if c == 1:
                nc.sync.dma_start(out=out0_v, in_=flat(park))

        def square_sum(rows, row, tile_index, parts):
            width = C // parts
            junk = junk_pool.tile([P, C], BF16, name="junk")
            for part in range(parts):
                col = 4 * tile_index + 2 + part
                nc.scalar.activation(
                    out=junk[:, part * width : (part + 1) * width],
                    in_=rows[:, part * width : (part + 1) * width],
                    func=ACT.Square,
                    accum_out=stats[:, row, col : col + 1],
                )

        def group_sums(row):
            sums = tp_pool.tile([P, H * 4], F32, name="bank")
            nc.tensor.matmul(
                out=sums[:], lhsT=group_mean[:].rearrange("p b q -> p (b q)"), rhs=stats[:, row, :], start=True, stop=True
            )
            return sums

        sums_of = {}
        moments = {}
        small = {}

        def edge_sums(s):
            if s in range(STEPS):
                sums_of[s] = group_sums(s)

        def take_moments(s):
            if s not in range(STEPS + 1):
                return
            moments[s] = small_pool.tile([P, 2, H], F32, name="moments")
            nc.vector.tensor_reduce(
                out=moments[s][:], in_=sums_of[s][:].rearrange("p (h k t) -> p k h t", k=2, t=2), axis=AX.X, op=ALU.add
            )

        def square_means(s):
            if s not in range(STEPS + 1):
                return
            small[s, "square"] = small_pool.tile([P, H], F32, name="sq_mean")
            nc.vector.tensor_tensor(
                out=small[s, "square"][:], in0=moments[s][:, 0], in1=moments[s][:, 0], op=ALU.mult
            )

        def variances(s):
            if s not in range(STEPS + 1):
                return
            small[s, "var"] = small_pool.tile([P, H], F32, name="var")
            nc.vector.tensor_tensor(
                out=small[s, "var"][:], in0=moments[s][:, 1], in1=small[s, "square"][:], op=ALU.subtract
            )

        def deviations(s):
            if s not in range(STEPS + 1):
                return
            safe = small_pool.tile([P, H], F32, name="safe")
            nc.vector.tensor_scalar(
                out=safe[:], in0=small[s, "var"][:], scalar1=0.0, scalar2=EPS, op0=ALU.max, op1=ALU.add
            )
            small[s, "rstd"] = small_pool.tile([P, H], F32, name="rstd")
            nc.gpsimd.tensor_tensor(out=small[s, "rstd"][:], in0=safe[:], in1=minus_half[:], op=ALU.pow)

        def scales(s):
            if s not in range(STEPS + 1):
                return
            small[s, "scale"] = small_pool.tile([P, H], F32, name="scale")
            nc.vector.tensor_tensor(
                out=small[s, "scale"][:], in0=small[s, "rstd"][:], in1=gain[:, H * s : H * s + H], op=ALU.mult
            )

        def drifts(s):
            if s not in range(STEPS + 1):
                return
            small[s, "drift"] = small_pool.tile([P, H], F32, name="drift")
            nc.vector.tensor_tensor(
                out=small[s, "drift"][:], in0=moments[s][:, 0], in1=small[s, "scale"][:], op=ALU.mult
            )

        def offsets(s):
            if s not in range(STEPS + 1):
                return
            offset = small_pool.tile([P, H], F32, name="offset")
            nc.vector.tensor_tensor(
                out=offset[:], in0=shift[:, H * s : H * s + H], in1=small[s, "drift"][:], op=ALU.subtract
            )
            coeffs[s] = (small[s, "scale"], offset)

        def normalise(s, h):
            if s not in range(STEPS):
                return
            scale, offset = coeffs[s]
            shared = h == H - 1 and s not in (0, Q + 1)
            width = C - SCALAR_COLS if shared else C
            nc.vector.tensor_scalar(
                out=msgs[s][:, h, :width],
                in0=msgs[s][:, h, :width],
                scalar1=scale[:, h : h + 1],
                scalar2=offset[:, h : h + 1],
                op0=ALU.mult,
                op1=ALU.add,
            )
            if width < C:
                nc.scalar.activation(
                    out=msgs[s][:, h, width:],
                    in_=msgs[s][:, h, width:],
                    func=ACT.Identity,
                    scale=scale[:, h : h + 1],
                    bias=offset[:, h : h + 1],
                )

        def node_sum_terms(c):
            for h in range(H):
                acc = mm_pool.tile([P, BANK], F32, name="acc")
                product(ux, wu, h, c, acc, nc.vector.tensor_copy)

        def pieces(s):
            count = QUARTERS if s == STEPS - 1 else H
            return [slice(i * W // count, (i + 1) * W // count) for i in range(count)]

        def half_pieces(s, h):
            cols = pieces(s)
            return cols[h * len(cols) // H : (h + 1) * len(cols) // H]

        def finish_edge(s, h):
            if s not in range(STEPS):
                return
            for cols in half_pieces(s, h):
                nc.vector.scalar_tensor_tensor(
                    out=flat(msgs[s])[:, cols],
                    in0=flat(msgs[s])[:, cols],
                    scalar=0.0,
                    in1=flat(edge_tiles[s])[:, cols],
                    op0=ALU.max,
                    op1=ALU.add,
                )
            if h < H - 1:
                return
            q = s % Q
            nc.sync.dma_start(out=out1_v[:, s // Q, q * W : (q + 1) * W], in_=flat(msgs[s]))

        def weights_of(s):
            if s not in range(STEPS):
                return
            gates[s] = gate_pool.tile([P, H, C], F32, name="gate")
            gate = flat(gates[s])
            for cols in pieces(s):
                nc.scalar.activation(out=gate[:, cols], in_=flat(msgs[s])[:, cols], func=ACT.Tanh, scale=0.5)
                nc.scalar.activation(out=gate[:, cols], in_=gate[:, cols], func=ACT.Exp, scale=0.5)

        def load_values(s):
            if s not in range(STEPS):
                return
            vt = value_pool.tile([P, H, C], F32, name="vt")
            nc.sync.dma_start(out=flat(vt), in_=parked_v[:, s % Q, :].unsqueeze(1).to_broadcast([N, Q, W]))
            values[s] = vt

        def weigh_values(s, h, parts=1, part=0):
            if s not in range(STEPS):
                return
            width = C // parts
            for cols in (half_pieces(s, h) if parts == 1 else [slice(h * C + part * width, h * C + (part + 1) * width)]):
                nc.vector.tensor_tensor(
                    out=flat(values[s])[:, cols], in0=flat(values[s])[:, cols], in1=flat(gates[s])[:, cols], op=ALU.mult
                )

        def sum_over_j(label, s, tile):
            if s not in range(STEPS):
                return
            half, q = divmod(s, Q)
            per_bank = BANK // P
            if q == 0:
                sums_t[label, half] = [
                    acc_pool.tile([P, per_bank, P], F32, name=label + str(b)) for b in range(C // BANK)
                ]
            for h in range(H):
                for chunk in range(CHUNKS):
                    b, place = divmod(chunk, per_bank)
                    nc.tensor.matmul(
                        out=sums_t[label, half][b][:, place, :],
                        lhsT=tile[:, h, chunk * P : (chunk + 1) * P],
                        rhs=ident[:],
                        is_transpose=True,
                        start=q == 0 and h == 0 and place == 0,
                        stop=q == Q - 1 and h == H - 1 and place == per_bank - 1,
                    )

        def finish_sums(label, s):
            if s not in (Q - 1, STEPS - 1):
                return
            half = s // Q
            pieces_t = [bank[:].rearrange("p k r -> p (k r)") for bank in sums_t[label, half]]
            if half == 0:
                t = keep.tile([P, C], F32, name=label + "_t")
                for b in range(C // BANK):
                    cols = slice(b * BANK, (b + 1) * BANK)
                    nc.scalar.copy(out=t[:, cols], in_=pieces_t[b])
                    pieces_t[b] = t[:, cols]
            totals[label, half] = pieces_t

        transpose_edge(0)
        group_edge(0)
        quantise_edge(0)
        node_product(ax, wa, 0, nc.scalar.copy)
        repeat_nodes(0)
        for n in range(MM_BANKS):
            fill_message_bank(n)
        node_product(ax, wa, 1, nc.scalar.copy)
        load_edge(PREFETCH)
        for k in (0, 1):
            evacuate(0, k)
            fill_message_bank(k + MM_BANKS)
        transpose_edge(1)
        group_edge(1)
        for q in (1, 2, 3):
            repeat_nodes(q)
        for k in (2, 3):
            evacuate(0, k)
        for q in (4, 5, 6):
            repeat_nodes(q)
        park_values(0)
        quantise_edge(1)
        for k in (2, 3):
            fill_message_bank(k + MM_BANKS)
        load_edge(1 + PREFETCH)
        for k in (0, 1):
            evacuate(1, k)
            fill_message_bank(QUARTERS + k + MM_BANKS)
        for h in range(H):
            square_sum(msgs[0][:, h, :], 0, h, 1)
        park_values(1)
        transpose_edge(2)
        group_edge(2)
        edge_sums(0)
        for k in (2, 3):
            evacuate(1, k)
        repeat_nodes(7)
        take_moments(0)
        square_means(0)
        quantise_edge(2)
        variances(0)
        load_values(0)
        load_values(1)
        for k in (2, 3):
            fill_message_bank(QUARTERS + k + MM_BANKS)
        for h in range(H):
            square_sum(msgs[1][:, h, :], 1, h, 1)
        deviations(0)
        scales(0)
        transpose_edge(3)
        group_edge(3)
        drifts(0)
        edge_sums(1)
        offsets(0)
        for h in range(H):
            normalise(0, h)
            finish_edge(0, h)
        weights_of(0)
        transpose_edge(4)
        for t in range(2, STEPS):
            load_edge(t + PREFETCH)
            take_moments(t - 1)
            evacuate(t, 0)
            fill_message_bank(QUARTERS * t + MM_BANKS)
            square_means(t - 1)
            evacuate(t, 1)
            fill_message_bank(QUARTERS * t + 1 + MM_BANKS)
            variances(t - 1)
            quantise_edge(t + 1)
            deviations(t - 1)
            load_values(t)
            weigh_values(t - 2, 0)
            sum_over_j("den", t - 2, gates.get(t - 2))
            square_sum(msgs[t][:, 0, :], t, 0, 1)
            for k in (2, 3):
                evacuate(t, k)
            fill_message_bank(QUARTERS * t + 2 + MM_BANKS)
            scales(t - 1)
            weigh_values(t - 2, 1, 2, 0)
            drifts(t - 1)
            weigh_values(t - 2, 1, 2, 1)
            group_edge(t + 2)
            square_sum(msgs[t][:, 1, :], t, 1, 1)
            offsets(t - 1)
            for h in range(H):
                normalise(t - 1, h)
            sum_over_j("num", t - 2, values.get(t - 2))
            fill_message_bank(QUARTERS * t + 3 + MM_BANKS)
            edge_sums(t)
            transpose_edge(t + 3)
            finish_edge(t - 1, 0)
            finish_edge(t - 1, 1)
            weights_of(t - 1)
            for label in ("den", "num"):
                finish_sums(label, t - 2)
        take_moments(STEPS - 1)
        square_means(STEPS - 1)
        variances(STEPS - 1)
        deviations(STEPS - 1)
        node_sum_terms(0)
        scales(STEPS - 1)
        drifts(STEPS - 1)
        offsets(STEPS - 1)
        for h in range(H):
            normalise(STEPS - 1, h)
            finish_edge(STEPS - 1, h)
        weights_of(STEPS - 1)
        for s in (STEPS - 2, STEPS - 1):
            for h in range(H):
                weigh_values(s, h)
            if s == STEPS - 2:
                node_sum_terms(1)
            for label, tiles in (("den", gates), ("num", values)):
                sum_over_j(label, s, tiles[s])
                finish_sums(label, s)

        y = msg_pool.tile([P, H, C], F32, name="msg")
        act = gate_pool.tile([P, H, C], F32, name="gate")
        quo = keep.tile([P, H, C], F32, name="quo")
        node_quarters = [(half, k, slice(k * BANK, (k + 1) * BANK)) for half in range(H) for k in range(C // BANK)]
        for half, k, cols in node_quarters:
            nc.scalar.activation(
                out=quo[:, half, cols], in_=totals["den", half][k], func=ACT.Abs_reciprocal_sqrt, scale=float(N)
            )
            nc.scalar.activation(out=quo[:, half, cols], in_=quo[:, half, cols], func=ACT.Square)

        def quotient_back(half, k, cols):
            nc.vector.tensor_tensor(
                out=quo[:, half, cols], in0=totals["num", half][k], in1=quo[:, half, cols], op=ALU.mult
            )
            back = mm_pool.tile([P, BANK], F32, name="acc")
            for place in range(BANK // P):
                nc.tensor.transpose(
                    out=back[:, place * P : (place + 1) * P],
                    in_=quo[:, half, k * BANK + place * P : k * BANK + (place + 1) * P],
                    identity=ident[:],
                )
            return back

        def node_sums(half, k, cols, back):
            nc.vector.scalar_tensor_tensor(
                out=y[:, half, cols],
                in0=back[:],
                scalar=1.0,
                in1=ux[:, half, cols],
                op0=ALU.mult,
                op1=ALU.add,
                accum_out=stats[:, STEPS, 4 * half + k : 4 * half + k + 1],
            )
            nc.scalar.activation(
                out=act[:, half, cols],
                in_=y[:, half, cols],
                func=ACT.Square,
                accum_out=stats[:, STEPS, 4 * half + 2 + k : 4 * half + 3 + k],
            )

        backs = [quotient_back(*node_quarters[0])]
        for i, part in enumerate(node_quarters):
            if i + 1 < len(node_quarters):
                backs.append(quotient_back(*node_quarters[i + 1]))
            node_sums(*part, backs[i])
        sums_of[STEPS] = group_sums(STEPS)
        take_moments(STEPS)
        square_means(STEPS)
        variances(STEPS)
        small[STEPS, "rstd"] = small_pool.tile([P, H], F32, name="rstd")
        nc.scalar.activation(
            out=small[STEPS, "rstd"][:], in_=small[STEPS, "var"][:], func=ACT.Abs_reciprocal_sqrt, bias=EPS
        )
        scales(STEPS)
        drifts(STEPS)
        offsets(STEPS)
        scale, offset = coeffs[STEPS]
        for half, k, cols in node_quarters:
            nc.scalar.activation(
                out=act[:, half, cols],
                in_=y[:, half, cols],
                func=ACT.Relu,
                scale=scale[:, half : half + 1],
                bias=offset[:, half : half + 1],
            )
            nc.vector.tensor_tensor(out=y[:, half, cols], in0=y[:, half, cols], in1=act[:, half, cols], op=ALU.add)
            nc.sync.dma_start(out=out0_v[:, half * C + k * BANK : half * C + (k + 1) * BANK], in_=y[:, half, cols])
